import numpy as np
import ml_dtypes


def mxq(x, axis, fmt="e4m3"):
    dtype, down = {"e4m3": (ml_dtypes.float8_e4m3fn, 7), "e5m2": (ml_dtypes.float8_e5m2, 14)}[fmt]
    v = np.moveaxis(np.asarray(x, np.float32).astype(ml_dtypes.bfloat16).astype(np.float64), axis, -1)
    blocks = v.reshape(v.shape[:-1] + (-1, 32))
    amax = np.abs(blocks).max(-1, keepdims=True)
    byte = np.maximum(np.where(amax > 0, np.frexp(amax)[1] - 1 + 127, 0) - down, 1)
    scale = np.exp2(byte - 127.0)
    codes = (blocks / scale).astype(np.float32).astype(dtype).astype(np.float64)
    return np.moveaxis((codes * scale).reshape(v.shape), -1, axis)


WIDE = False


def mx_kscale(k):
    if not WIDE:
        return np.ones(k)
    levels = np.array([10, -10, 5, -5, 0])
    if k % 512:
        return np.exp2(np.random.permutation(np.resize(levels, k // 32))).repeat(32)
    a = np.empty((k // 512, 16))
    for p in range(k // 512):
        a[p, :8] = np.random.permutation(np.resize(levels, 8))
        for g in range(8):
            far = levels[np.abs(levels - a[p, g]) >= 10]
            a[p, g + 8] = far[np.random.randint(len(far))]
    return np.exp2(a.ravel()).repeat(32)


BF16 = ml_dtypes.bfloat16


def bf(x):
    return np.asarray(x, np.float32).astype(BF16)


def f64(x):
    return np.asarray(x).astype(np.float64)


B, D_IN, D_H, W_RANK, U_RANK = 4096, 1024, 1024, 512, 512


def sigmoid(v):
    return 1.0 / (1.0 + np.exp(-v))


def setup_inputs():
    s, t = mx_kscale(W_RANK), mx_kscale(U_RANK)
    return {
        "wx_r": bf(np.random.standard_normal((B, W_RANK)) * s),
        "uh_r": bf(np.random.standard_normal((B, U_RANK)) * t),
        "state": bf(np.random.standard_normal((B, D_H))),
        "W2": bf(np.random.standard_normal((D_H, W_RANK)) * 0.7 / np.sqrt(W_RANK) / s),
        "U2": bf(np.random.standard_normal((D_H, U_RANK)) * 0.7 / np.sqrt(U_RANK) / t),
        "bias_gate": bf(1.0 + 0.5 * np.random.standard_normal((1, D_H))),
        "bias_update": bf(1.0 + 0.5 * np.random.standard_normal((1, D_H))),
        "zeta": bf(1.0 + 0.1 * np.random.standard_normal((1, 1))),
        "nu": bf(-1.5 + 0.1 * np.random.standard_normal((1, 1))),
    }


def reference(wx_r, uh_r, state, W2, U2, bias_gate, bias_update, zeta, nu):
    wx = mxq(f64(wx_r), 1, "e4m3") @ mxq(f64(W2), 1, "e4m3").T
    uh = mxq(f64(uh_r), 1, "e4m3") @ mxq(f64(U2), 1, "e4m3").T
    pre = wx + uh
    z = sigmoid(pre + f64(bias_gate))
    h_cand = np.tanh(pre + f64(bias_update))
    return z * f64(state) + (sigmoid(f64(zeta)) * (1.0 - z) + sigmoid(f64(nu))) * h_cand

@@ -1,0 +1,288 @@
+from contextlib import ExitStack
+
+import concourse.mybir as mybir
+from concourse.masks import make_identity
+
+F32 = mybir.dt.float32
+BF16 = mybir.dt.bfloat16
+U32 = mybir.dt.uint32
+U8 = mybir.dt.uint8
+FP8X4 = mybir.dt.float8_e4m3fn_x4
+ACT = mybir.ActivationFunctionType
+ALU = mybir.AluOpType
+
+P = 128
+PACK = 4
+BATCH, RANK, HIDDEN = 4096, 512, 1024
+ROWS = 512
+BLOCKS = ROWS // P
+CHUNKS = BATCH // ROWS
+HALVES = HIDDEN // ROWS
+UNITS = CHUNKS * HALVES
+WORDS = RANK // 2
+RAW_BUFS = 6
+FIRST_STEPS = 8
+LEAD = 14
+TINY = 1e-30
+
+FLOPS = 2 * BATCH * HIDDEN * (2 * RANK)
+
+
+def tile_fastgrnncudacell_pa_t_kernel(
+    tc, wx_r, uh_r, state, W2, U2, bias_gate, bias_update, zeta, nu, out
+):
+    nc = tc.nc
+    with ExitStack() as ctx:
+        const = ctx.enter_context(tc.tile_pool(name="const", bufs=1))
+        raw_pool = ctx.enter_context(tc.tile_pool(name="raw", bufs=RAW_BUFS))
+        grouped_pool = ctx.enter_context(tc.tile_pool(name="grouped", bufs=3))
+        moving_pool = ctx.enter_context(tc.tile_pool(name="moving", bufs=2))
+        state_pool = ctx.enter_context(tc.tile_pool(name="state", bufs=3))
+        gates_pool = ctx.enter_context(tc.tile_pool(name="gates", bufs=4))
+        out_pool = ctx.enter_context(tc.tile_pool(name="outp", bufs=2))
+        shift_pool = ctx.enter_context(tc.tile_pool(name="shift", bufs=2))
+        psum_pre = ctx.enter_context(tc.psum_pool(name="psum_pre", bufs=2))
+        psum_fwd = ctx.enter_context(tc.psum_pool(name="psum_fwd", bufs=1))
+        psum_back = ctx.enter_context(tc.psum_pool(name="psum_back", bufs=5))
+        ctx.enter_context(tc.manual_schedule())
+
+        batch_view = "(c p i) d -> c p (i d)"
+        state_v = state.rearrange(batch_view, p=P, i=BLOCKS)
+        out_v = out.rearrange(batch_view, p=P, i=BLOCKS)
+        weight_view = "(h q p) k -> h p q k"
+        sources = {
+            "wx": wx_r.rearrange(batch_view, p=P, i=BLOCKS),
+            "uh": uh_r.rearrange(batch_view, p=P, i=BLOCKS),
+            "w2": W2.rearrange(weight_view, q=BLOCKS, p=P),
+            "u2": U2.rearrange(weight_view, q=BLOCKS, p=P),
+        }
+        operands = [("w2", 0), ("wx", 0), ("u2", 0), ("uh", 0), ("w2", 1), ("u2", 1)]
+        for c in range(1, CHUNKS):
+            operands.extend([("wx", c), ("uh", c)])
+        total_steps = 2 * len(operands)
+
+        raw = {}
+        grouped = {}
+        codes = {}
+        scales = {}
+
+        def load_operand(k):
+            kind, index = operands[k]
+            raw[k] = raw_pool.tile([P, BLOCKS * RANK], BF16, name="raw", tag="raw")
+            if kind in ("wx", "uh"):
+                nc.sync.dma_start(out=raw[k][:], in_=sources[kind][index])
+            else:
+                nc.sync.dma_start(
+                    out=raw[k][:].rearrange("p (q k) -> p q k", q=BLOCKS),
+                    in_=sources[kind][index],
+                )
+
+        def load_state(c):
+            state_sb[c] = state_pool.tile([P, BLOCKS * HIDDEN], BF16, name="state_sb", tag="state_sb")
+            nc.sync.dma_start(out=state_sb[c][:], in_=state_v[c])
+
+        def transpose_step(s, on_vector):
+            k, a = divmod(s, 2)
+            if a == 0:
+                grouped[k] = grouped_pool.tile(
+                    [P, ROWS * PACK], BF16, name="grouped", tag="grouped", align_bytes=64
+                )
+            words = raw[k][:].bitcast(F32)
+            flipped = psum_fwd.tile([P, 2 * 2 * P], F32, name="flipped", tag="flipped")
+            for v in range(2):
+                for j in range(2):
+                    block = 2 * a + j
+                    nc.tensor.transpose(
+                        flipped[:, (2 * v + j) * P : (2 * v + j + 1) * P],
+                        words[:, block * WORDS + v : (block + 1) * WORDS : 2],
+                        ident[:],
+                    )
+            dst = grouped[k][:].bitcast(F32).rearrange("p (n v) -> p n v", v=2)
+            dst = dst[:, 2 * a * P : 2 * (a + 1) * P, :]
+            src = flipped[:].rearrange("p (v n) -> p n v", v=2)
+            if on_vector:
+                nc.vector.tensor_copy(out=dst, in_=src)
+            else:
+                nc.scalar.copy(out=dst, in_=src)
+            if a == 1 and k + RAW_BUFS < len(operands):
+                load_operand(k + RAW_BUFS)
+
+        def quantise(k):
+            kind, index = operands[k]
+            if kind in ("wx", "uh"):
+                pool, tag = moving_pool, kind
+            else:
+                pool, tag = const, "%s%d" % (kind, index)
+            codes[operands[k]] = pool.tile(
+                [P, ROWS], U32, name="codes_" + tag, tag="codes_" + tag, align_bytes=64
+            )
+            scales[operands[k]] = pool.tile(
+                [P, ROWS], U8, name="scales_" + tag, tag="scales_" + tag, align_bytes=64
+            )
+            nc.vector.quantize_mx(
+                out=codes[operands[k]][:].bitcast(FP8X4),
+                scales=scales[operands[k]][:],
+                in_=grouped[k][:],
+            )
+
+        gate_t = {}
+        cand_t = {}
+        state_sb = {}
+        out_sb = {}
+
+        def project(u, q):
+            c, h = divmod(u, HALVES)
+            if q == 0:
+                gate_t[u] = gates_pool.tile([P, BLOCKS * ROWS], F32, name="gate_t", tag="gate_t")
+                cand_t[u] = gates_pool.tile([P, BLOCKS * ROWS], F32, name="cand_t", tag="cand_t")
+            m = BLOCKS * h + q
+            pre = psum_pre.tile([P, ROWS], F32, name="pre", tag="pre")
+            pairs = ((("w2", h), ("wx", c)), (("u2", h), ("uh", c)))
+            for n, (weight, moving) in enumerate(pairs):
+                nc.tensor.matmul_mx(
+                    out=pre[:],
+                    lhsT=codes[weight][:, q * P : (q + 1) * P].bitcast(FP8X4),
+                    lhsT_scale=scales[weight][:, q * P : (q + 1) * P],
+                    rhs=codes[moving][:].bitcast(FP8X4),
+                    rhs_scale=scales[moving][:],
+                    start=(n == 0),
+                    stop=(n == 1),
+                )
+            cols = slice(q * ROWS, (q + 1) * ROWS)
+            nc.scalar.activation(
+                out=gate_t[u][:, cols], in_=pre[:], func=ACT.Sigmoid,
+                bias=bias_t[:, m : m + 1], scale=1.0,
+            )
+            nc.scalar.activation(
+                out=cand_t[u][:, cols], in_=pre[:], func=ACT.Tanh,
+                bias=bias_t[:, 2 * BLOCKS + m : 2 * BLOCKS + m + 1], scale=1.0,
+            )
+
+        def candidate_term(u, a):
+            cols = slice(2 * a * ROWS, (2 * a + 1) * ROWS)
+            nc.vector.scalar_tensor_tensor(
+                out=cand_t[u][:, cols], in0=gate_t[u][:, cols], scalar=kappa[:, 0:1],
+                in1=cand_t[u][:, cols], op0=ALU.subtract, op1=ALU.mult,
+            )
+            cols = slice((2 * a + 1) * ROWS, (2 * a + 2) * ROWS)
+            shifted = shift_pool.tile([P, ROWS], F32, name="shifted", tag="shifted")
+            nc.gpsimd.tensor_scalar(
+                out=shifted[:], in0=gate_t[u][:, cols], scalar1=one[:, 0:1],
+                scalar2=neg_kappa[:, 0:1], op0=ALU.mult, op1=ALU.add,
+            )
+            nc.gpsimd.tensor_tensor(
+                out=cand_t[u][:, cols], in0=shifted[:], in1=cand_t[u][:, cols], op=ALU.mult
+            )
+
+        def transpose_back(source, a):
+            banks = []
+            for j in range(2):
+                i = 2 * a + j
+                bank = psum_back.tile([P, ROWS], F32, name="bank", tag="bank")
+                for q in range(BLOCKS):
+                    nc.tensor.transpose(
+                        bank[:, q * P : (q + 1) * P],
+                        source[:, q * ROWS + i * P : q * ROWS + (i + 1) * P],
+                        ident[:],
+                    )
+                banks.append(bank)
+            return banks
+
+        def mix(u, a, banks):
+            c, h = divmod(u, HALVES)
+            if h == 0 and a == 0:
+                out_sb[c] = out_pool.tile([P, BLOCKS * HIDDEN], F32, name="out_sb", tag="out_sb")
+            spans = [
+                slice((2 * a + j) * HIDDEN + h * ROWS, (2 * a + j) * HIDDEN + (h + 1) * ROWS)
+                for j in range(2)
+            ]
+            for j in range(2):
+                nc.vector.tensor_tensor(
+                    out=out_sb[c][:, spans[j]], in0=banks[j][:], in1=state_sb[c][:, spans[j]],
+                    op=ALU.mult,
+                )
+            for j in range(2):
+                nc.vector.scalar_tensor_tensor(
+                    out=out_sb[c][:, spans[j]], in0=banks[2 + j][:], scalar=neg_sz[:, 0:1],
+                    in1=out_sb[c][:, spans[j]], op0=ALU.mult, op1=ALU.add,
+                )
+            if h == HALVES - 1:
+                done = slice(2 * a * HIDDEN, 2 * (a + 1) * HIDDEN)
+                nc.sync.dma_start(out=out_v[c][:, done], in_=out_sb[c][:, done])
+
+        for k in range(4):
+            load_operand(k)
+        zeta_sb = const.tile([P, 1], BF16, name="zeta_sb")
+        nu_sb = const.tile([P, 1], BF16, name="nu_sb")
+        bias_rows = const.tile([P, P], BF16, name="bias_rows")
+        nc.gpsimd.memset(bias_rows[:], 0.0)
+        nc.scalar.dma_start(out=zeta_sb[:], in_=zeta.to_broadcast([P, 1]))
+        nc.scalar.dma_start(out=nu_sb[:], in_=nu.to_broadcast([P, 1]))
+        row_view = "o (m p) -> (o m) p"
+        nc.scalar.dma_start(out=bias_rows[0 : 2 * BLOCKS, :], in_=bias_gate.rearrange(row_view, p=P))
+        nc.scalar.dma_start(
+            out=bias_rows[2 * BLOCKS : 4 * BLOCKS, :], in_=bias_update.rearrange(row_view, p=P)
+        )
+        for k in range(4, RAW_BUFS):
+            load_operand(k)
+        load_state(0)
+
+        ident = const.tile([P, P], F32, name="ident")
+        make_identity(nc, ident[:])
+
+        sz = const.tile([P, 1], F32, name="sz")
+        sn = const.tile([P, 1], F32, name="sn")
+        inv_sz = const.tile([P, 1], F32, name="inv_sz")
+        kappa = const.tile([P, 1], F32, name="kappa")
+        neg_sz = const.tile([P, 1], F32, name="neg_sz")
+        nc.scalar.activation(out=sz[:], in_=zeta_sb[:], func=ACT.Sigmoid)
+        nc.scalar.activation(out=sn[:], in_=nu_sb[:], func=ACT.Sigmoid)
+        nc.vector.tensor_scalar_max(out=sz[:], in0=sz[:], scalar1=TINY)
+        nc.vector.reciprocal(out=inv_sz[:], in_=sz[:])
+        nc.vector.tensor_add(out=kappa[:], in0=sz[:], in1=sn[:])
+        nc.vector.tensor_mul(out=kappa[:], in0=kappa[:], in1=inv_sz[:])
+        nc.vector.tensor_scalar_mul(out=neg_sz[:], in0=sz[:], scalar1=-1.0)
+        neg_kappa = const.tile([P, 1], F32, name="neg_kappa")
+        one = const.tile([P, 1], F32, name="one")
+        nc.vector.tensor_scalar_mul(out=neg_kappa[:], in0=kappa[:], scalar1=-1.0)
+        nc.vector.memset(one[:], 1.0)
+
+        bias_rows_f = const.tile([P, P], F32, name="bias_rows_f")
+        bias_t = const.tile([P, 4 * BLOCKS], F32, name="bias_t")
+        nc.vector.tensor_copy(out=bias_rows_f[:], in_=bias_rows[:])
+        bias_ps = psum_fwd.tile([P, 2 * 2 * P], F32, name="bias_ps", tag="flipped")
+        nc.tensor.transpose(bias_ps[:, 0:P], bias_rows_f[:], ident[:])
+        nc.vector.tensor_copy(out=bias_t[:], in_=bias_ps[:, 0 : 4 * BLOCKS])
+
+        for s in range(FIRST_STEPS):
+            transpose_step(s, on_vector=(s % 2 == 1))
+            if s % 2 == 1:
+                quantise(s // 2)
+        steps_done = FIRST_STEPS
+
+        for t in range(2 * (UNITS + 2)):
+            u, a = divmod(t, 2)
+            if t % (2 * HALVES) == 0 and t // (2 * HALVES) + 1 < CHUNKS:
+                load_state(t // (2 * HALVES) + 1)
+            banks = []
+            if u < UNITS:
+                project(u, 2 * a)
+            if u >= 2:
+                banks.extend(transpose_back(gate_t[u - 2], a))
+            if u < UNITS:
+                project(u, 2 * a + 1)
+            if u >= 2:
+                banks.extend(transpose_back(cand_t[u - 2], a))
+            steps_due = min(total_steps, steps_done + 2, t + 1 + LEAD)
+            finished = []
+            while steps_done < steps_due:
+                transpose_step(steps_done, on_vector=(u < 2))
+                if steps_done % 2 == 1:
+                    finished.append(steps_done // 2)
+                steps_done += 1
+            if u >= 2:
+                mix(u - 2, a, banks)
+            if 1 <= u <= UNITS:
+                candidate_term(u - 1, a)
+            for k in finished:
+                quantise(k)

@@ -17,13 +17,12 @@ BATCH, RANK, HIDDEN = 4096, 512, 1024
 ROWS = 512
 BLOCKS = ROWS // P
 CHUNKS = BATCH // ROWS
-HALVES = HIDDEN // ROWS
-UNITS = CHUNKS * HALVES
+SPAN = 2 * P
+SPANS = HIDDEN // SPAN
+STEPS = CHUNKS * SPANS
 WORDS = RANK // 2
-RAW_BUFS = 6
-FIRST_STEPS = 8
-LEAD = 14
-TINY = 1e-30
+STORE_SPANS = 2
+SZ_FLOOR = 2.0 ** -13
 
 FLOPS = 2 * BATCH * HIDDEN * (2 * RANK)
 
@@ -34,255 +33,348 @@ def tile_fastgrnncudacell_pa_t_kernel(
     nc = tc.nc
     with ExitStack() as ctx:
         const = ctx.enter_context(tc.tile_pool(name="const", bufs=1))
-        raw_pool = ctx.enter_context(tc.tile_pool(name="raw", bufs=RAW_BUFS))
+        raw_w_pool = ctx.enter_context(tc.tile_pool(name="raw_w", bufs=8))
+        raw_x_pool = ctx.enter_context(tc.tile_pool(name="raw_x", bufs=6))
         grouped_pool = ctx.enter_context(tc.tile_pool(name="grouped", bufs=3))
-        moving_pool = ctx.enter_context(tc.tile_pool(name="moving", bufs=2))
+        moving_pool = ctx.enter_context(tc.tile_pool(name="moving", bufs=3))
         state_pool = ctx.enter_context(tc.tile_pool(name="state", bufs=3))
-        gates_pool = ctx.enter_context(tc.tile_pool(name="gates", bufs=4))
-        out_pool = ctx.enter_context(tc.tile_pool(name="outp", bufs=2))
-        shift_pool = ctx.enter_context(tc.tile_pool(name="shift", bufs=2))
-        psum_pre = ctx.enter_context(tc.psum_pool(name="psum_pre", bufs=2))
+        gates_pool = ctx.enter_context(tc.tile_pool(name="gates", bufs=3))
+        out_pool = ctx.enter_context(tc.tile_pool(name="outp", bufs=4))
+        psum_pre = ctx.enter_context(tc.psum_pool(name="psum_pre", bufs=4))
         psum_fwd = ctx.enter_context(tc.psum_pool(name="psum_fwd", bufs=1))
-        psum_back = ctx.enter_context(tc.psum_pool(name="psum_back", bufs=5))
+        psum_state = ctx.enter_context(tc.psum_pool(name="psum_state", bufs=1))
+        psum_back = ctx.enter_context(tc.psum_pool(name="psum_back", bufs=2))
         ctx.enter_context(tc.manual_schedule())
 
         batch_view = "(c p i) d -> c p (i d)"
         state_v = state.rearrange(batch_view, p=P, i=BLOCKS)
-        out_v = out.rearrange(batch_view, p=P, i=BLOCKS)
-        weight_view = "(h q p) k -> h p q k"
+        out_v = out.rearrange("(c p i) d -> c p i d", p=P, i=BLOCKS)
+        weight_view = "(j p e) k -> j p (e k)"
         sources = {
             "wx": wx_r.rearrange(batch_view, p=P, i=BLOCKS),
             "uh": uh_r.rearrange(batch_view, p=P, i=BLOCKS),
-            "w2": W2.rearrange(weight_view, q=BLOCKS, p=P),
-            "u2": U2.rearrange(weight_view, q=BLOCKS, p=P),
+            "w2": W2.rearrange(weight_view, p=P, e=2),
+            "u2": U2.rearrange(weight_view, p=P, e=2),
         }
-        operands = [("w2", 0), ("wx", 0), ("u2", 0), ("uh", 0), ("w2", 1), ("u2", 1)]
-        for c in range(1, CHUNKS):
-            operands.extend([("wx", c), ("uh", c)])
-        total_steps = 2 * len(operands)
+        blocks_of = {"wx": BLOCKS, "uh": BLOCKS, "w2": 2, "u2": 2}
 
         raw = {}
         grouped = {}
         codes = {}
         scales = {}
+        state_sb = {}
+        out_sb = {}
 
-        def load_operand(k):
-            kind, index = operands[k]
-            raw[k] = raw_pool.tile([P, BLOCKS * RANK], BF16, name="raw", tag="raw")
+        def load_operand(kind, index):
             if kind in ("wx", "uh"):
-                nc.sync.dma_start(out=raw[k][:], in_=sources[kind][index])
+                tile = raw_x_pool.tile([P, BLOCKS * RANK], BF16, name="raw_x", tag="raw_x")
             else:
-                nc.sync.dma_start(
-                    out=raw[k][:].rearrange("p (q k) -> p q k", q=BLOCKS),
-                    in_=sources[kind][index],
-                )
+                tile = raw_w_pool.tile([P, 2 * RANK], BF16, name="raw_w", tag="raw_w")
+            raw[kind, index] = tile
+            nc.sync.dma_start(out=tile[:], in_=sources[kind][index])
 
         def load_state(c):
             state_sb[c] = state_pool.tile([P, BLOCKS * HIDDEN], BF16, name="state_sb", tag="state_sb")
             nc.sync.dma_start(out=state_sb[c][:], in_=state_v[c])
 
-        def transpose_step(s, on_vector):
-            k, a = divmod(s, 2)
-            if a == 0:
-                grouped[k] = grouped_pool.tile(
-                    [P, ROWS * PACK], BF16, name="grouped", tag="grouped", align_bytes=64
-                )
-            words = raw[k][:].bitcast(F32)
-            flipped = psum_fwd.tile([P, 2 * 2 * P], F32, name="flipped", tag="flipped")
+        def bank_tile(tag):
+            if tag == "fwd":
+                return psum_fwd.tile([P, ROWS], F32, name="fwd", tag="fwd")
+            if tag == "st":
+                return psum_state.tile([P, ROWS], F32, name="st", tag="st")
+            if tag == "back":
+                return psum_back.tile([P, ROWS], F32, name="back", tag="back")
+            return psum_pre.tile([P, ROWS], F32, name="pre", tag="pre")
+
+        flipped = {}
+
+        def flip(kind, index, a, tag):
+            words = raw[kind, index][:].bitcast(F32)
+            bank = bank_tile(tag)
             for v in range(2):
-                for j in range(2):
-                    block = 2 * a + j
+                for b in range(2):
+                    block = 2 * a + b
                     nc.tensor.transpose(
-                        flipped[:, (2 * v + j) * P : (2 * v + j + 1) * P],
+                        bank[:, (2 * v + b) * P : (2 * v + b + 1) * P],
                         words[:, block * WORDS + v : (block + 1) * WORDS : 2],
                         ident[:],
                     )
-            dst = grouped[k][:].bitcast(F32).rearrange("p (n v) -> p n v", v=2)
+            flipped[kind, index, a] = bank
+
+        def group(kind, index, a, on_vector):
+            if a == 0:
+                grouped[kind, index] = grouped_pool.tile(
+                    [P, ROWS * PACK], BF16, name="grouped", tag="grouped", align_bytes=64
+                )
+            dst = grouped[kind, index][:].bitcast(F32).rearrange("p (n v) -> p n v", v=2)
             dst = dst[:, 2 * a * P : 2 * (a + 1) * P, :]
-            src = flipped[:].rearrange("p (v n) -> p n v", v=2)
+            src = flipped[kind, index, a][:].rearrange("p (v n) -> p n v", v=2)
             if on_vector:
                 nc.vector.tensor_copy(out=dst, in_=src)
             else:
                 nc.scalar.copy(out=dst, in_=src)
-            if a == 1 and k + RAW_BUFS < len(operands):
-                load_operand(k + RAW_BUFS)
 
-        def quantise(k):
-            kind, index = operands[k]
-            if kind in ("wx", "uh"):
-                pool, tag = moving_pool, kind
-            else:
-                pool, tag = const, "%s%d" % (kind, index)
-            codes[operands[k]] = pool.tile(
-                [P, ROWS], U32, name="codes_" + tag, tag="codes_" + tag, align_bytes=64
-            )
-            scales[operands[k]] = pool.tile(
-                [P, ROWS], U8, name="scales_" + tag, tag="scales_" + tag, align_bytes=64
-            )
+        def quantise(kind, index):
+            rows = blocks_of[kind] * P
+            pool = moving_pool if kind in ("wx", "uh") else const
+            tag = kind if kind in ("wx", "uh") else "%s%d" % (kind, index)
+            codes[kind, index] = pool.tile([P, rows], U32, name="c_" + tag, tag="c_" + tag, align_bytes=64)
+            scales[kind, index] = pool.tile([P, rows], U8, name="s_" + tag, tag="s_" + tag, align_bytes=64)
             nc.vector.quantize_mx(
-                out=codes[operands[k]][:].bitcast(FP8X4),
-                scales=scales[operands[k]][:],
-                in_=grouped[k][:],
+                out=codes[kind, index][:].bitcast(FP8X4),
+                scales=scales[kind, index][:],
+                in_=grouped[kind, index][:, 0 : rows * PACK],
             )
 
+        pre = {}
         gate_t = {}
         cand_t = {}
-        state_sb = {}
-        out_sb = {}
+        state_ps = {}
+        back = {}
 
-        def project(u, q):
-            c, h = divmod(u, HALVES)
-            if q == 0:
-                gate_t[u] = gates_pool.tile([P, BLOCKS * ROWS], F32, name="gate_t", tag="gate_t")
-                cand_t[u] = gates_pool.tile([P, BLOCKS * ROWS], F32, name="cand_t", tag="cand_t")
-            m = BLOCKS * h + q
-            pre = psum_pre.tile([P, ROWS], F32, name="pre", tag="pre")
-            pairs = ((("w2", h), ("wx", c)), (("u2", h), ("uh", c)))
-            for n, (weight, moving) in enumerate(pairs):
-                nc.tensor.matmul_mx(
-                    out=pre[:],
-                    lhsT=codes[weight][:, q * P : (q + 1) * P].bitcast(FP8X4),
-                    lhsT_scale=scales[weight][:, q * P : (q + 1) * P],
-                    rhs=codes[moving][:].bitcast(FP8X4),
-                    rhs_scale=scales[moving][:],
-                    start=(n == 0),
-                    stop=(n == 1),
+        def project(r):
+            c, j = divmod(r, SPANS)
+            for e in range(2):
+                pre[r, e] = bank_tile("pre")
+                pairs = ((("w2", j), ("wx", c)), (("u2", j), ("uh", c)))
+                for n, (weight, moving) in enumerate(pairs):
+                    nc.tensor.matmul_mx(
+                        out=pre[r, e][:],
+                        lhsT=codes[weight][:, e * P : (e + 1) * P].bitcast(FP8X4),
+                        lhsT_scale=scales[weight][:, e * P : (e + 1) * P],
+                        rhs=codes[moving][:].bitcast(FP8X4),
+                        rhs_scale=scales[moving][:],
+                        start=(n == 0),
+                        stop=(n == 1),
+                    )
+
+        def activate(r, e, which):
+            j = r % SPANS
+            cols = slice(e * ROWS, (e + 1) * ROWS)
+            if which == "tanh":
+                column = 2 * SPANS * e + SPANS + j
+                nc.scalar.activation(
+                    out=cand_t[r][:, cols], in_=pre[r, e][:], func=ACT.Tanh,
+                    bias=bias_t[:, column : column + 1], scale=1.0,
                 )
-            cols = slice(q * ROWS, (q + 1) * ROWS)
-            nc.scalar.activation(
-                out=gate_t[u][:, cols], in_=pre[:], func=ACT.Sigmoid,
-                bias=bias_t[:, m : m + 1], scale=1.0,
-            )
-            nc.scalar.activation(
-                out=cand_t[u][:, cols], in_=pre[:], func=ACT.Tanh,
-                bias=bias_t[:, 2 * BLOCKS + m : 2 * BLOCKS + m + 1], scale=1.0,
+            else:
+                column = 2 * SPANS * e + j
+                nc.scalar.activation(
+                    out=gate_t[r][:, cols], in_=pre[r, e][:], func=ACT.Sigmoid,
+                    bias=bias_t[:, column : column + 1], scale=1.0,
+                )
+
+        def flip_state(r):
+            c, j = divmod(r, SPANS)
+            words = state_sb[c][:].bitcast(F32)
+            state_ps[r] = bank_tile("st")
+            for i in range(BLOCKS):
+                start = i * (HIDDEN // 2) + j * P
+                nc.tensor.transpose(
+                    state_ps[r][:, i * P : (i + 1) * P], words[:, start : start + P], ident[:]
+                )
+
+        def subtract(r):
+            view = "p (e n) -> p e n"
+            nc.vector.scalar_tensor_tensor(
+                out=cand_t[r][:].rearrange(view, e=2),
+                in0=cand_t[r][:].rearrange(view, e=2),
+                scalar=neg_sz[:, 0:1],
+                in1=state_ps[r][:].bitcast(BF16).rearrange("p (n e) -> p e n", e=2),
+                op0=ALU.mult, op1=ALU.add,
             )
 
-        def candidate_term(u, a):
-            cols = slice(2 * a * ROWS, (2 * a + 1) * ROWS)
+        def product_vector(r):
+            cols = slice(ROWS, 2 * ROWS)
             nc.vector.scalar_tensor_tensor(
-                out=cand_t[u][:, cols], in0=gate_t[u][:, cols], scalar=kappa[:, 0:1],
-                in1=cand_t[u][:, cols], op0=ALU.subtract, op1=ALU.mult,
+                out=cand_t[r][:, cols], in0=gate_t[r][:, cols], scalar=kappa[:, 0:1],
+                in1=cand_t[r][:, cols], op0=ALU.subtract, op1=ALU.mult,
             )
-            cols = slice((2 * a + 1) * ROWS, (2 * a + 2) * ROWS)
-            shifted = shift_pool.tile([P, ROWS], F32, name="shifted", tag="shifted")
+
+        def product_gpsimd(r):
+            cols = slice(0, ROWS)
             nc.gpsimd.tensor_scalar(
-                out=shifted[:], in0=gate_t[u][:, cols], scalar1=one[:, 0:1],
+                out=gate_t[r][:, cols], in0=gate_t[r][:, cols], scalar1=one[:, 0:1],
                 scalar2=neg_kappa[:, 0:1], op0=ALU.mult, op1=ALU.add,
             )
             nc.gpsimd.tensor_tensor(
-                out=cand_t[u][:, cols], in0=shifted[:], in1=cand_t[u][:, cols], op=ALU.mult
+                out=cand_t[r][:, cols], in0=gate_t[r][:, cols], in1=cand_t[r][:, cols], op=ALU.mult
             )
 
-        def transpose_back(source, a):
-            banks = []
-            for j in range(2):
-                i = 2 * a + j
-                bank = psum_back.tile([P, ROWS], F32, name="bank", tag="bank")
-                for q in range(BLOCKS):
-                    nc.tensor.transpose(
-                        bank[:, q * P : (q + 1) * P],
-                        source[:, q * ROWS + i * P : q * ROWS + (i + 1) * P],
-                        ident[:],
-                    )
-                banks.append(bank)
-            return banks
+        def flip_back(r):
+            for b in range(2):
+                back[r, b] = bank_tile("back")
+                for i in range(2):
+                    for e in range(2):
+                        first = e * ROWS + (2 * b + i) * P
+                        nc.tensor.transpose(
+                            back[r, b][:, (2 * e + i) * P : (2 * e + i + 1) * P],
+                            cand_t[r][:, first : first + P],
+                            ident[:],
+                        )
 
-        def mix(u, a, banks):
-            c, h = divmod(u, HALVES)
-            if h == 0 and a == 0:
-                out_sb[c] = out_pool.tile([P, BLOCKS * HIDDEN], F32, name="out_sb", tag="out_sb")
-            spans = [
-                slice((2 * a + j) * HIDDEN + h * ROWS, (2 * a + j) * HIDDEN + (h + 1) * ROWS)
-                for j in range(2)
-            ]
-            for j in range(2):
-                nc.vector.tensor_tensor(
-                    out=out_sb[c][:, spans[j]], in0=banks[j][:], in1=state_sb[c][:, spans[j]],
-                    op=ALU.mult,
+        def mix(r, b):
+            c, j = divmod(r, SPANS)
+            group_first, half = divmod(j, STORE_SPANS)
+            if half == 0 and b == 0:
+                out_sb[c, group_first] = out_pool.tile(
+                    [P, BLOCKS * STORE_SPANS * SPAN], F32, name="out_sb", tag="out_sb"
                 )
-            for j in range(2):
-                nc.vector.scalar_tensor_tensor(
-                    out=out_sb[c][:, spans[j]], in0=banks[2 + j][:], scalar=neg_sz[:, 0:1],
-                    in1=out_sb[c][:, spans[j]], op0=ALU.mult, op1=ALU.add,
-                )
-            if h == HALVES - 1:
-                done = slice(2 * a * HIDDEN, 2 * (a + 1) * HIDDEN)
-                nc.sync.dma_start(out=out_v[c][:, done], in_=out_sb[c][:, done])
+            block_view = "q (i d) -> q i d"
+            pair_view = "q i (p e) -> q i p e"
+            blocks = slice(2 * b, 2 * b + 2)
+            state_part = state_sb[c][:].rearrange(block_view, i=BLOCKS)
+            state_part = state_part[:, blocks, j * SPAN : (j + 1) * SPAN]
+            out_part = out_sb[c, group_first][:].rearrange(block_view, i=BLOCKS)
+            out_part = out_part[:, blocks, half * SPAN : (half + 1) * SPAN]
+            nc.vector.scalar_tensor_tensor(
+                out=out_part.rearrange(pair_view, e=2),
+                in0=state_part.rearrange(pair_view, e=2),
+                scalar=kappa[:, 0:1],
+                in1=back[r, b][:].rearrange("q (e i p) -> q i p e", i=2, e=2),
+                op0=ALU.mult, op1=ALU.add,
+            )
 
-        for k in range(4):
-            load_operand(k)
+        def store(r):
+            c, j = divmod(r, SPANS)
+            group_first = j // STORE_SPANS
+            first = group_first * STORE_SPANS * SPAN
+            nc.sync.dma_start(
+                out=out_v[c][:, :, first : first + STORE_SPANS * SPAN],
+                in_=out_sb[c, group_first][:].rearrange("q (i d) -> q i d", i=BLOCKS),
+            )
+
+        load_operand("w2", 0)
+        load_operand("wx", 0)
+        load_operand("u2", 0)
+        load_operand("uh", 0)
         zeta_sb = const.tile([P, 1], BF16, name="zeta_sb")
         nu_sb = const.tile([P, 1], BF16, name="nu_sb")
-        bias_rows = const.tile([P, P], BF16, name="bias_rows")
+        bias_rows = const.tile([P, SPAN], BF16, name="bias_rows")
         nc.gpsimd.memset(bias_rows[:], 0.0)
         nc.scalar.dma_start(out=zeta_sb[:], in_=zeta.to_broadcast([P, 1]))
         nc.scalar.dma_start(out=nu_sb[:], in_=nu.to_broadcast([P, 1]))
-        row_view = "o (m p) -> (o m) p"
-        nc.scalar.dma_start(out=bias_rows[0 : 2 * BLOCKS, :], in_=bias_gate.rearrange(row_view, p=P))
+        row_view = "o (j m) -> (o j) m"
+        nc.scalar.dma_start(out=bias_rows[0:SPANS, :], in_=bias_gate.rearrange(row_view, m=SPAN))
         nc.scalar.dma_start(
-            out=bias_rows[2 * BLOCKS : 4 * BLOCKS, :], in_=bias_update.rearrange(row_view, p=P)
+            out=bias_rows[SPANS : 2 * SPANS, :], in_=bias_update.rearrange(row_view, m=SPAN)
         )
-        for k in range(4, RAW_BUFS):
-            load_operand(k)
-        load_state(0)
-
         ident = const.tile([P, P], F32, name="ident")
         make_identity(nc, ident[:])
+        load_operand("w2", 1)
+        load_operand("u2", 1)
+        load_state(0)
+        load_operand("w2", 2)
+        load_operand("u2", 2)
+        load_operand("wx", 1)
+        load_operand("w2", 3)
+        load_operand("u2", 3)
+        load_operand("uh", 1)
 
         sz = const.tile([P, 1], F32, name="sz")
         sn = const.tile([P, 1], F32, name="sn")
         inv_sz = const.tile([P, 1], F32, name="inv_sz")
         kappa = const.tile([P, 1], F32, name="kappa")
         neg_sz = const.tile([P, 1], F32, name="neg_sz")
-        nc.scalar.activation(out=sz[:], in_=zeta_sb[:], func=ACT.Sigmoid)
-        nc.scalar.activation(out=sn[:], in_=nu_sb[:], func=ACT.Sigmoid)
-        nc.vector.tensor_scalar_max(out=sz[:], in0=sz[:], scalar1=TINY)
-        nc.vector.reciprocal(out=inv_sz[:], in_=sz[:])
-        nc.vector.tensor_add(out=kappa[:], in0=sz[:], in1=sn[:])
-        nc.vector.tensor_mul(out=kappa[:], in0=kappa[:], in1=inv_sz[:])
-        nc.vector.tensor_scalar_mul(out=neg_sz[:], in0=sz[:], scalar1=-1.0)
         neg_kappa = const.tile([P, 1], F32, name="neg_kappa")
         one = const.tile([P, 1], F32, name="one")
-        nc.vector.tensor_scalar_mul(out=neg_kappa[:], in0=kappa[:], scalar1=-1.0)
+        nc.scalar.activation(out=sz[:], in_=zeta_sb[:], func=ACT.Sigmoid)
+        nc.scalar.activation(out=sn[:], in_=nu_sb[:], func=ACT.Sigmoid)
         nc.vector.memset(one[:], 1.0)
+        nc.vector.tensor_add(out=sn[:], in0=sz[:], in1=sn[:])
+        nc.vector.tensor_scalar_max(out=sz[:], in0=sz[:], scalar1=SZ_FLOOR)
+        nc.vector.reciprocal(out=inv_sz[:], in_=sz[:])
+        nc.vector.tensor_scalar_mul(out=neg_sz[:], in0=sz[:], scalar1=-1.0)
+        nc.vector.tensor_mul(out=kappa[:], in0=sn[:], in1=inv_sz[:])
+        nc.vector.tensor_scalar_mul(out=neg_kappa[:], in0=kappa[:], scalar1=-1.0)
 
-        bias_rows_f = const.tile([P, P], F32, name="bias_rows_f")
-        bias_t = const.tile([P, 4 * BLOCKS], F32, name="bias_t")
+        flip("w2", 0, 0, "back")
+        group("w2", 0, 0, on_vector=True)
+        flip("wx", 0, 0, "back")
+        group("wx", 0, 0, on_vector=False)
+        flip("wx", 0, 1, "st")
+        quantise("w2", 0)
+        group("wx", 0, 1, on_vector=True)
+        flip("u2", 0, 0, "fwd")
+        group("u2", 0, 0, on_vector=False)
+        flip("uh", 0, 0, "back")
+        quantise("wx", 0)
+        group("uh", 0, 0, on_vector=False)
+        flip("uh", 0, 1, "back")
+        quantise("u2", 0)
+        group("uh", 0, 1, on_vector=True)
+
+        bias_rows_f = const.tile([P, SPAN], F32, name="bias_rows_f")
+        bias_t = const.tile([P, 4 * SPANS], F32, name="bias_t")
         nc.vector.tensor_copy(out=bias_rows_f[:], in_=bias_rows[:])
-        bias_ps = psum_fwd.tile([P, 2 * 2 * P], F32, name="bias_ps", tag="flipped")
-        nc.tensor.transpose(bias_ps[:, 0:P], bias_rows_f[:], ident[:])
-        nc.vector.tensor_copy(out=bias_t[:], in_=bias_ps[:, 0 : 4 * BLOCKS])
+        bias_ps = bank_tile("st")
+        for e in range(2):
+            nc.tensor.transpose(bias_ps[:, e * P : (e + 1) * P], bias_rows_f[:, e::2], ident[:])
+        nc.scalar.copy(
+            out=bias_t[:].rearrange("p (e m) -> p e m", e=2),
+            in_=bias_ps[:, 0:SPAN].rearrange("p (e m) -> p e m", e=2)[:, :, 0 : 2 * SPANS],
+        )
+        quantise("uh", 0)
+        flip("w2", 1, 0, "fwd")
+        group("w2", 1, 0, on_vector=True)
+        project(0)
+        flip("u2", 1, 0, "back")
+        group("u2", 1, 0, on_vector=True)
+        quantise("w2", 1)
+        quantise("u2", 1)
 
-        for s in range(FIRST_STEPS):
-            transpose_step(s, on_vector=(s % 2 == 1))
-            if s % 2 == 1:
-                quantise(s // 2)
-        steps_done = FIRST_STEPS
+        def preparations(r):
+            if r < 2:
+                return [("w2", r + 2, 0), ("u2", r + 2, 0), ("wx", 1, r)]
+            if r == 2:
+                return [("uh", 1, 0), ("uh", 1, 1)]
+            c, k = divmod(r - 3, SPANS)
+            if c + 2 < CHUNKS:
+                return [("wx" if k < 2 else "uh", c + 2, k % 2)]
+            return []
 
-        for t in range(2 * (UNITS + 2)):
-            u, a = divmod(t, 2)
-            if t % (2 * HALVES) == 0 and t // (2 * HALVES) + 1 < CHUNKS:
-                load_state(t // (2 * HALVES) + 1)
-            banks = []
-            if u < UNITS:
-                project(u, 2 * a)
-            if u >= 2:
-                banks.extend(transpose_back(gate_t[u - 2], a))
-            if u < UNITS:
-                project(u, 2 * a + 1)
-            if u >= 2:
-                banks.extend(transpose_back(cand_t[u - 2], a))
-            steps_due = min(total_steps, steps_done + 2, t + 1 + LEAD)
-            finished = []
-            while steps_done < steps_due:
-                transpose_step(steps_done, on_vector=(u < 2))
-                if steps_done % 2 == 1:
-                    finished.append(steps_done // 2)
-                steps_done += 1
-            if u >= 2:
-                mix(u - 2, a, banks)
-            if 1 <= u <= UNITS:
-                candidate_term(u - 1, a)
-            for k in finished:
-                quantise(k)
+        for r in range(STEPS + 2):
+            c, j = divmod(r, SPANS)
+            if j == 0 and c + 1 < CHUNKS:
+                load_state(c + 1)
+                if c + 2 < CHUNKS:
+                    load_operand("wx", c + 2)
+                    load_operand("uh", c + 2)
+            prep = preparations(r)
+            if r >= 2:
+                flip_back(r - 2)
+            for n, (kind, index, a) in enumerate(prep):
+                flip(kind, index, a, "fwd" if n == 0 or r >= 2 else "back")
+                if r < 3:
+                    group(kind, index, a, on_vector=True)
+            if r < STEPS:
+                gate_t[r] = gates_pool.tile([P, 2 * ROWS], F32, name="gate_t", tag="gate_t")
+                cand_t[r] = gates_pool.tile([P, 2 * ROWS], F32, name="cand_t", tag="cand_t")
+                activate(r, 0, "tanh")
+                activate(r, 1, "tanh")
+                activate(r, 1, "sigmoid")
+            if r >= 3:
+                for kind, index, a in prep:
+                    group(kind, index, a, on_vector=False)
+            if r < STEPS:
+                activate(r, 0, "sigmoid")
+            if 1 <= r <= STEPS:
+                subtract(r - 1)
+                product_gpsimd(r - 1)
+            if r < STEPS:
+                flip_state(r)
+            for kind, index, a in prep:
+                if r < 3 and a == blocks_of[kind] // 2 - 1:
+                    quantise(kind, index)
+            if r + 1 < STEPS:
+                project(r + 1)
+            if r >= 2:
+                mix(r - 2, 0)
+                mix(r - 2, 1)
+                if (r - 2) % STORE_SPANS == STORE_SPANS - 1:
+                    store(r - 2)
+            if 1 <= r <= STEPS:
+                product_vector(r - 1)
+            for kind, index, a in prep:
+                if r >= 3 and a == 1:
+                    quantise(kind, index)

@@ -22,6 +22,8 @@ SPANS = HIDDEN // SPAN
 STEPS = CHUNKS * SPANS
 WORDS = RANK // 2
 STORE_SPANS = 2
+G_COLS = 576
+V_COLS = 2 * ROWS - G_COLS
 SZ_FLOOR = 2.0 ** -13
 
 FLOPS = 2 * BATCH * HIDDEN * (2 * RANK)
@@ -38,11 +40,11 @@ def tile_fastgrnncudacell_pa_t_kernel(
         grouped_pool = ctx.enter_context(tc.tile_pool(name="grouped", bufs=3))
         moving_pool = ctx.enter_context(tc.tile_pool(name="moving", bufs=3))
         state_pool = ctx.enter_context(tc.tile_pool(name="state", bufs=3))
-        gates_pool = ctx.enter_context(tc.tile_pool(name="gates", bufs=3))
+        gates_pool = ctx.enter_context(tc.tile_pool(name="gates", bufs=5))
         out_pool = ctx.enter_context(tc.tile_pool(name="outp", bufs=4))
-        psum_pre = ctx.enter_context(tc.psum_pool(name="psum_pre", bufs=4))
+        psum_pre = ctx.enter_context(tc.psum_pool(name="psum_pre", bufs=3))
         psum_fwd = ctx.enter_context(tc.psum_pool(name="psum_fwd", bufs=1))
-        psum_state = ctx.enter_context(tc.psum_pool(name="psum_state", bufs=1))
+        psum_state = ctx.enter_context(tc.psum_pool(name="psum_state", bufs=2))
         psum_back = ctx.enter_context(tc.psum_pool(name="psum_back", bufs=2))
         ctx.enter_context(tc.manual_schedule())
 
@@ -132,21 +134,20 @@ def tile_fastgrnncudacell_pa_t_kernel(
         state_ps = {}
         back = {}
 
-        def project(r):
+        def project(r, e):
             c, j = divmod(r, SPANS)
-            for e in range(2):
-                pre[r, e] = bank_tile("pre")
-                pairs = ((("w2", j), ("wx", c)), (("u2", j), ("uh", c)))
-                for n, (weight, moving) in enumerate(pairs):
-                    nc.tensor.matmul_mx(
-                        out=pre[r, e][:],
-                        lhsT=codes[weight][:, e * P : (e + 1) * P].bitcast(FP8X4),
-                        lhsT_scale=scales[weight][:, e * P : (e + 1) * P],
-                        rhs=codes[moving][:].bitcast(FP8X4),
-                        rhs_scale=scales[moving][:],
-                        start=(n == 0),
-                        stop=(n == 1),
-                    )
+            pre[r, e] = bank_tile("pre")
+            pairs = ((("w2", j), ("wx", c)), (("u2", j), ("uh", c)))
+            for n, (weight, moving) in enumerate(pairs):
+                nc.tensor.matmul_mx(
+                    out=pre[r, e][:],
+                    lhsT=codes[weight][:, e * P : (e + 1) * P].bitcast(FP8X4),
+                    lhsT_scale=scales[weight][:, e * P : (e + 1) * P],
+                    rhs=codes[moving][:].bitcast(FP8X4),
+                    rhs_scale=scales[moving][:],
+                    start=(n == 0),
+                    stop=(n == 1),
+                )
 
         def activate(r, e, which):
             j = r % SPANS
@@ -185,20 +186,22 @@ def tile_fastgrnncudacell_pa_t_kernel(
             )
 
         def product_vector(r):
-            cols = slice(ROWS, 2 * ROWS)
+            cols = slice(0, V_COLS)
             nc.vector.scalar_tensor_tensor(
                 out=cand_t[r][:, cols], in0=gate_t[r][:, cols], scalar=kappa[:, 0:1],
                 in1=cand_t[r][:, cols], op0=ALU.subtract, op1=ALU.mult,
             )
 
-        def product_gpsimd(r):
-            cols = slice(0, ROWS)
+        def shift_gpsimd(r):
             nc.gpsimd.tensor_scalar(
-                out=gate_t[r][:, cols], in0=gate_t[r][:, cols], scalar1=one[:, 0:1],
+                out=gate_t[r - 1][:, 0:G_COLS], in0=gate_t[r][:, V_COLS:], scalar1=one[:, 0:1],
                 scalar2=neg_kappa[:, 0:1], op0=ALU.mult, op1=ALU.add,
             )
+
+        def product_gpsimd(r):
             nc.gpsimd.tensor_tensor(
-                out=cand_t[r][:, cols], in0=gate_t[r][:, cols], in1=cand_t[r][:, cols], op=ALU.mult
+                out=cand_t[r][:, V_COLS:], in0=gate_t[r - 1][:, 0:G_COLS], in1=cand_t[r][:, V_COLS:],
+                op=ALU.mult,
             )
 
         def flip_back(r):
@@ -244,10 +247,10 @@ def tile_fastgrnncudacell_pa_t_kernel(
                 in_=out_sb[c, group_first][:].rearrange("q (i d) -> q i d", i=BLOCKS),
             )
 
-        load_operand("w2", 0)
         load_operand("wx", 0)
-        load_operand("u2", 0)
         load_operand("uh", 0)
+        load_operand("w2", 0)
+        load_operand("u2", 0)
         zeta_sb = const.tile([P, 1], BF16, name="zeta_sb")
         nu_sb = const.tile([P, 1], BF16, name="nu_sb")
         bias_rows = const.tile([P, SPAN], BF16, name="bias_rows")
@@ -288,52 +291,54 @@ def tile_fastgrnncudacell_pa_t_kernel(
         nc.vector.tensor_mul(out=kappa[:], in0=sn[:], in1=inv_sz[:])
         nc.vector.tensor_scalar_mul(out=neg_kappa[:], in0=kappa[:], scalar1=-1.0)
 
-        flip("w2", 0, 0, "back")
-        group("w2", 0, 0, on_vector=True)
-        flip("wx", 0, 0, "back")
-        group("wx", 0, 0, on_vector=False)
-        flip("wx", 0, 1, "st")
-        quantise("w2", 0)
-        group("wx", 0, 1, on_vector=True)
-        flip("u2", 0, 0, "fwd")
-        group("u2", 0, 0, on_vector=False)
-        flip("uh", 0, 0, "back")
-        quantise("wx", 0)
-        group("uh", 0, 0, on_vector=False)
-        flip("uh", 0, 1, "back")
-        quantise("u2", 0)
-        group("uh", 0, 1, on_vector=True)
-
         bias_rows_f = const.tile([P, SPAN], F32, name="bias_rows_f")
         bias_t = const.tile([P, 4 * SPANS], F32, name="bias_t")
         nc.vector.tensor_copy(out=bias_rows_f[:], in_=bias_rows[:])
-        bias_ps = bank_tile("st")
+
+        flip("wx", 0, 0, "back")
+        group("wx", 0, 0, on_vector=False)
+        flip("wx", 0, 1, "back")
+        group("wx", 0, 1, on_vector=True)
+        bias_ps = bank_tile("pre")
         for e in range(2):
             nc.tensor.transpose(bias_ps[:, e * P : (e + 1) * P], bias_rows_f[:, e::2], ident[:])
         nc.scalar.copy(
             out=bias_t[:].rearrange("p (e m) -> p e m", e=2),
             in_=bias_ps[:, 0:SPAN].rearrange("p (e m) -> p e m", e=2)[:, :, 0 : 2 * SPANS],
         )
+        flip("uh", 0, 0, "st")
+        group("uh", 0, 0, on_vector=False)
+        quantise("wx", 0)
+        flip("uh", 0, 1, "st")
+        group("uh", 0, 1, on_vector=True)
+        flip("w2", 0, 0, "fwd")
+        group("w2", 0, 0, on_vector=False)
         quantise("uh", 0)
-        flip("w2", 1, 0, "fwd")
-        group("w2", 1, 0, on_vector=True)
-        project(0)
-        flip("u2", 1, 0, "back")
+        flip("u2", 0, 0, "back")
+        group("u2", 0, 0, on_vector=True)
+        quantise("w2", 0)
+        flip("w2", 1, 0, "back")
+        group("w2", 1, 0, on_vector=False)
+        quantise("u2", 0)
+        flip("u2", 1, 0, "fwd")
         group("u2", 1, 0, on_vector=True)
+        project(0, 0)
+        project(0, 1)
         quantise("w2", 1)
         quantise("u2", 1)
 
         def preparations(r):
             if r < 2:
-                return [("w2", r + 2, 0), ("u2", r + 2, 0), ("wx", 1, r)]
+                return [("w2", r + 2, 0, True), ("u2", r + 2, 0, False), ("wx", 1, r, r == 0)]
             if r == 2:
-                return [("uh", 1, 0), ("uh", 1, 1)]
+                return [("uh", 1, 0, False), ("uh", 1, 1, True)]
             c, k = divmod(r - 3, SPANS)
             if c + 2 < CHUNKS:
-                return [("wx" if k < 2 else "uh", c + 2, k % 2)]
+                return [("wx" if k < 2 else "uh", c + 2, k % 2, False)]
             return []
 
-        for r in range(STEPS + 2):
+        gate_t[-1] = gates_pool.tile([P, 2 * ROWS], F32, name="gate_t", tag="gate_t")
+        for r in range(STEPS + 3):
             c, j = divmod(r, SPANS)
             if j == 0 and c + 1 < CHUNKS:
                 load_state(c + 1)
@@ -341,40 +346,42 @@ def tile_fastgrnncudacell_pa_t_kernel(
                     load_operand("wx", c + 2)
                     load_operand("uh", c + 2)
             prep = preparations(r)
-            if r >= 2:
-                flip_back(r - 2)
-            for n, (kind, index, a) in enumerate(prep):
-                flip(kind, index, a, "fwd" if n == 0 or r >= 2 else "back")
-                if r < 3:
-                    group(kind, index, a, on_vector=True)
+            for n, (kind, index, a, on_vector) in enumerate(prep):
+                flip(kind, index, a, "back" if n > 0 else "fwd")
+            if r < STEPS:
+                flip_state(r)
+            if r >= 3:
+                flip_back(r - 3)
+            if r + 1 < STEPS:
+                project(r + 1, 0)
             if r < STEPS:
                 gate_t[r] = gates_pool.tile([P, 2 * ROWS], F32, name="gate_t", tag="gate_t")
                 cand_t[r] = gates_pool.tile([P, 2 * ROWS], F32, name="cand_t", tag="cand_t")
                 activate(r, 0, "tanh")
-                activate(r, 1, "tanh")
-                activate(r, 1, "sigmoid")
-            if r >= 3:
-                for kind, index, a in prep:
-                    group(kind, index, a, on_vector=False)
-            if r < STEPS:
                 activate(r, 0, "sigmoid")
+                activate(r, 1, "tanh")
+            for kind, index, a, on_vector in prep:
+                if not on_vector:
+                    group(kind, index, a, False)
+            if r < STEPS:
+                activate(r, 1, "sigmoid")
+            if r + 1 < STEPS:
+                project(r + 1, 1)
             if 1 <= r <= STEPS:
                 subtract(r - 1)
-                product_gpsimd(r - 1)
-            if r < STEPS:
-                flip_state(r)
-            for kind, index, a in prep:
-                if r < 3 and a == blocks_of[kind] // 2 - 1:
+                shift_gpsimd(r - 1)
+            if 2 <= r <= STEPS + 1:
+                product_gpsimd(r - 2)
+            for kind, index, a, on_vector in prep:
+                if on_vector:
+                    group(kind, index, a, True)
+            if r >= 3:
+                mix(r - 3, 0)
+                mix(r - 3, 1)
+                if (r - 3) % STORE_SPANS == STORE_SPANS - 1:
+                    store(r - 3)
+            for kind, index, a, on_vector in prep:
+                if a == blocks_of[kind] // 2 - 1:
                     quantise(kind, index)
-            if r + 1 < STEPS:
-                project(r + 1)
-            if r >= 2:
-                mix(r - 2, 0)
-                mix(r - 2, 1)
-                if (r - 2) % STORE_SPANS == STORE_SPANS - 1:
-                    store(r - 2)
             if 1 <= r <= STEPS:
                 product_vector(r - 1)
-            for kind, index, a in prep:
-                if r >= 3 and a == 1:
-                    quantise(kind, index)

@@ -350,10 +350,10 @@ def tile_fastgrnncudacell_pa_t_kernel(
                 flip(kind, index, a, "back" if n > 0 else "fwd")
             if r < STEPS:
                 flip_state(r)
-            if r >= 3:
-                flip_back(r - 3)
             if r + 1 < STEPS:
                 project(r + 1, 0)
+            if r >= 3:
+                flip_back(r - 3)
             if r < STEPS:
                 gate_t[r] = gates_pool.tile([P, 2 * ROWS], F32, name="gate_t", tag="gate_t")
                 cand_t[r] = gates_pool.tile([P, 2 * ROWS], F32, name="cand_t", tag="cand_t")

@@ -22,7 +22,7 @@ SPANS = HIDDEN // SPAN
 STEPS = CHUNKS * SPANS
 WORDS = RANK // 2
 STORE_SPANS = 2
-G_COLS = 576
+G_COLS = 384
 V_COLS = 2 * ROWS - G_COLS
 SZ_FLOOR = 2.0 ** -13
 

@@ -21,9 +21,9 @@ SPAN = 2 * P
 SPANS = HIDDEN // SPAN
 STEPS = CHUNKS * SPANS
 WORDS = RANK // 2
-STORE_SPANS = 2
-G_COLS = 384
+G_COLS = 512
 V_COLS = 2 * ROWS - G_COLS
+S_COLS = 192
 SZ_FLOOR = 2.0 ** -13
 
 FLOPS = 2 * BATCH * HIDDEN * (2 * RANK)
@@ -185,8 +185,11 @@ def tile_fastgrnncudacell_pa_t_kernel(
                 op0=ALU.mult, op1=ALU.add,
             )
 
+        def vector_only(r):
+            return r == 0
+
         def product_vector(r):
-            cols = slice(0, V_COLS)
+            cols = slice(0, 2 * ROWS if vector_only(r) else V_COLS)
             nc.vector.scalar_tensor_tensor(
                 out=cand_t[r][:, cols], in0=gate_t[r][:, cols], scalar=kappa[:, 0:1],
                 in1=cand_t[r][:, cols], op0=ALU.subtract, op1=ALU.mult,
@@ -194,8 +197,15 @@ def tile_fastgrnncudacell_pa_t_kernel(
 
         def shift_gpsimd(r):
             nc.gpsimd.tensor_scalar(
-                out=gate_t[r - 1][:, 0:G_COLS], in0=gate_t[r][:, V_COLS:], scalar1=one[:, 0:1],
+                out=gate_t[r - 1][:, 0 : G_COLS - S_COLS], in0=gate_t[r][:, V_COLS : 2 * ROWS - S_COLS],
+                scalar1=one[:, 0:1],
                 scalar2=neg_kappa[:, 0:1], op0=ALU.mult, op1=ALU.add,
+            )
+
+        def shift_scalar(r):
+            nc.scalar.activation(
+                out=gate_t[r - 1][:, G_COLS - S_COLS : G_COLS], in_=gate_t[r][:, 2 * ROWS - S_COLS :],
+                func=ACT.Identity, bias=neg_kappa[:, 0:1], scale=1.0,
             )
 
         def product_gpsimd(r):
@@ -216,12 +226,15 @@ def tile_fastgrnncudacell_pa_t_kernel(
                             ident[:],
                         )
 
+        def store_spans(c):
+            return 2 if c < CHUNKS - 1 else 1
+
         def mix(r, b):
             c, j = divmod(r, SPANS)
-            group_first, half = divmod(j, STORE_SPANS)
+            group_first, half = divmod(j, store_spans(c))
             if half == 0 and b == 0:
                 out_sb[c, group_first] = out_pool.tile(
-                    [P, BLOCKS * STORE_SPANS * SPAN], F32, name="out_sb", tag="out_sb"
+                    [P, BLOCKS * store_spans(c) * SPAN], F32, name="out_sb", tag="out_sb"
                 )
             block_view = "q (i d) -> q i d"
             pair_view = "q i (p e) -> q i p e"
@@ -240,12 +253,12 @@ def tile_fastgrnncudacell_pa_t_kernel(
 
         def store(r):
             c, j = divmod(r, SPANS)
-            group_first = j // STORE_SPANS
-            first = group_first * STORE_SPANS * SPAN
-            nc.sync.dma_start(
-                out=out_v[c][:, :, first : first + STORE_SPANS * SPAN],
-                in_=out_sb[c, group_first][:].rearrange("q (i d) -> q i d", i=BLOCKS),
-            )
+            spans = store_spans(c)
+            if (j + 1) % spans == 0:
+                nc.sync.dma_start(
+                    out=out_v[c][:, :, (j + 1 - spans) * SPAN : (j + 1) * SPAN],
+                    in_=out_sb[c, j // spans][:].rearrange("q (i d) -> q i d", i=BLOCKS),
+                )
 
         load_operand("wx", 0)
         load_operand("uh", 0)
@@ -337,7 +350,6 @@ def tile_fastgrnncudacell_pa_t_kernel(
                 return [("wx" if k < 2 else "uh", c + 2, k % 2, False)]
             return []
 
-        gate_t[-1] = gates_pool.tile([P, 2 * ROWS], F32, name="gate_t", tag="gate_t")
         for r in range(STEPS + 3):
             c, j = divmod(r, SPANS)
             if j == 0 and c + 1 < CHUNKS:
@@ -360,6 +372,8 @@ def tile_fastgrnncudacell_pa_t_kernel(
                 activate(r, 0, "tanh")
                 activate(r, 0, "sigmoid")
                 activate(r, 1, "tanh")
+            if 1 <= r <= STEPS and not vector_only(r - 1):
+                shift_scalar(r - 1)
             for kind, index, a, on_vector in prep:
                 if not on_vector:
                     group(kind, index, a, False)
@@ -369,8 +383,9 @@ def tile_fastgrnncudacell_pa_t_kernel(
                 project(r + 1, 1)
             if 1 <= r <= STEPS:
                 subtract(r - 1)
-                shift_gpsimd(r - 1)
-            if 2 <= r <= STEPS + 1:
+                if not vector_only(r - 1):
+                    shift_gpsimd(r - 1)
+            if 2 <= r <= STEPS + 1 and not vector_only(r - 2):
                 product_gpsimd(r - 2)
             for kind, index, a, on_vector in prep:
                 if on_vector:
@@ -378,8 +393,7 @@ def tile_fastgrnncudacell_pa_t_kernel(
             if r >= 3:
                 mix(r - 3, 0)
                 mix(r - 3, 1)
-                if (r - 3) % STORE_SPANS == STORE_SPANS - 1:
-                    store(r - 3)
+                store(r - 3)
             for kind, index, a, on_vector in prep:
                 if a == blocks_of[kind] // 2 - 1:
                     quantise(kind, index)

@@ -362,10 +362,10 @@ def tile_fastgrnncudacell_pa_t_kernel(
                 flip(kind, index, a, "back" if n > 0 else "fwd")
             if r < STEPS:
                 flip_state(r)
-            if r + 1 < STEPS:
-                project(r + 1, 0)
             if r >= 3:
                 flip_back(r - 3)
+            if r + 1 < STEPS:
+                project(r + 1, 0)
             if r < STEPS:
                 gate_t[r] = gates_pool.tile([P, 2 * ROWS], F32, name="gate_t", tag="gate_t")
                 cand_t[r] = gates_pool.tile([P, 2 * ROWS], F32, name="cand_t", tag="cand_t")

@@ -21,9 +21,10 @@ SPAN = 2 * P
 SPANS = HIDDEN // SPAN
 STEPS = CHUNKS * SPANS
 WORDS = RANK // 2
-G_COLS = 512
+G_COLS = 528
 V_COLS = 2 * ROWS - G_COLS
-S_COLS = 192
+S_COLS = 208
+WARM_PASSES = 5
 SZ_FLOOR = 2.0 ** -13
 
 FLOPS = 2 * BATCH * HIDDEN * (2 * RANK)
@@ -49,7 +50,7 @@ def tile_fastgrnncudacell_pa_t_kernel(
         ctx.enter_context(tc.manual_schedule())
 
         batch_view = "(c p i) d -> c p (i d)"
-        state_v = state.rearrange(batch_view, p=P, i=BLOCKS)
+        state_v = state.rearrange("(c p i) d -> c p i d", p=P, i=BLOCKS)
         out_v = out.rearrange("(c p i) d -> c p i d", p=P, i=BLOCKS)
         weight_view = "(j p e) k -> j p (e k)"
         sources = {
@@ -75,9 +76,24 @@ def tile_fastgrnncudacell_pa_t_kernel(
             raw[kind, index] = tile
             nc.sync.dma_start(out=tile[:], in_=sources[kind][index])
 
-        def load_state(c):
-            state_sb[c] = state_pool.tile([P, BLOCKS * HIDDEN], BF16, name="state_sb", tag="state_sb")
-            nc.sync.dma_start(out=state_sb[c][:], in_=state_v[c])
+        def state_spans(c):
+            return 2 if c == 0 else SPANS
+
+        def load_state(c, part):
+            width = state_spans(c) * SPAN
+            state_sb[c, part] = state_pool.tile(
+                [P, BLOCKS * width], BF16, name="state_sb", tag="state_sb%d" % state_spans(c)
+            )
+            nc.sync.dma_start(
+                out=state_sb[c, part][:].rearrange("q (i d) -> q i d", i=BLOCKS),
+                in_=state_v[c][:, :, part * width : (part + 1) * width],
+            )
+
+        def state_span(r):
+            c, j = divmod(r, SPANS)
+            part, k = divmod(j, state_spans(c))
+            tile = state_sb[c, part][:].rearrange("q (i d) -> q i d", i=BLOCKS)
+            return tile[:, :, k * SPAN : (k + 1) * SPAN]
 
         def bank_tile(tag):
             if tag == "fwd":
@@ -166,13 +182,10 @@ def tile_fastgrnncudacell_pa_t_kernel(
                 )
 
         def flip_state(r):
-            c, j = divmod(r, SPANS)
-            words = state_sb[c][:].bitcast(F32)
             state_ps[r] = bank_tile("st")
             for i in range(BLOCKS):
-                start = i * (HIDDEN // 2) + j * P
                 nc.tensor.transpose(
-                    state_ps[r][:, i * P : (i + 1) * P], words[:, start : start + P], ident[:]
+                    state_ps[r][:, i * P : (i + 1) * P], state_span(r)[:, i, :].bitcast(F32), ident[:]
                 )
 
         def subtract(r):
@@ -239,8 +252,7 @@ def tile_fastgrnncudacell_pa_t_kernel(
             block_view = "q (i d) -> q i d"
             pair_view = "q i (p e) -> q i p e"
             blocks = slice(2 * b, 2 * b + 2)
-            state_part = state_sb[c][:].rearrange(block_view, i=BLOCKS)
-            state_part = state_part[:, blocks, j * SPAN : (j + 1) * SPAN]
+            state_part = state_span(r)[:, blocks, :]
             out_part = out_sb[c, group_first][:].rearrange(block_view, i=BLOCKS)
             out_part = out_part[:, blocks, half * SPAN : (half + 1) * SPAN]
             nc.vector.scalar_tensor_tensor(
@@ -260,6 +272,9 @@ def tile_fastgrnncudacell_pa_t_kernel(
                     in_=out_sb[c, j // spans][:].rearrange("q (i d) -> q i d", i=BLOCKS),
                 )
 
+        zeros = const.tile([P, ROWS], BF16, name="zeros")
+        nc.vector.memset(zeros[:], 0.0)
+
         load_operand("wx", 0)
         load_operand("uh", 0)
         load_operand("w2", 0)
@@ -268,25 +283,59 @@ def tile_fastgrnncudacell_pa_t_kernel(
         nu_sb = const.tile([P, 1], BF16, name="nu_sb")
         bias_rows = const.tile([P, SPAN], BF16, name="bias_rows")
         nc.gpsimd.memset(bias_rows[:], 0.0)
-        nc.scalar.dma_start(out=zeta_sb[:], in_=zeta.to_broadcast([P, 1]))
-        nc.scalar.dma_start(out=nu_sb[:], in_=nu.to_broadcast([P, 1]))
         row_view = "o (j m) -> (o j) m"
         nc.scalar.dma_start(out=bias_rows[0:SPANS, :], in_=bias_gate.rearrange(row_view, m=SPAN))
         nc.scalar.dma_start(
             out=bias_rows[SPANS : 2 * SPANS, :], in_=bias_update.rearrange(row_view, m=SPAN)
         )
+        nc.scalar.dma_start(out=zeta_sb[:], in_=zeta.to_broadcast([P, 1]))
+        nc.scalar.dma_start(out=nu_sb[:], in_=nu.to_broadcast([P, 1]))
         ident = const.tile([P, P], F32, name="ident")
         make_identity(nc, ident[:])
         load_operand("w2", 1)
         load_operand("u2", 1)
-        load_state(0)
+        load_state(0, 0)
         load_operand("w2", 2)
         load_operand("u2", 2)
         load_operand("wx", 1)
         load_operand("w2", 3)
         load_operand("u2", 3)
+        load_state(0, 1)
         load_operand("uh", 1)
 
+        unused = const.tile([P, 1], F32, name="unused")
+        nc.scalar.activation(out=unused[:], in_=zeros[:, 0:1], func=ACT.Sigmoid)
+        warm_ps = bank_tile("pre")
+        for k in range(WARM_PASSES):
+            nc.tensor.matmul(out=warm_ps[:], lhsT=zeros[:, 0:P], rhs=zeros[:], start=True, stop=True)
+
+        flip("wx", 0, 0, "back")
+        group("wx", 0, 0, on_vector=False)
+        flip("wx", 0, 1, "back")
+        group("wx", 0, 1, on_vector=True)
+        flip("uh", 0, 0, "st")
+        group("uh", 0, 0, on_vector=False)
+        quantise("wx", 0)
+        flip("uh", 0, 1, "st")
+        group("uh", 0, 1, on_vector=True)
+        bias_rows_f = const.tile([P, SPAN], F32, name="bias_rows_f")
+        bias_t = const.tile([P, 4 * SPANS], F32, name="bias_t")
+        nc.vector.tensor_copy(out=bias_rows_f[:], in_=bias_rows[:])
+        flip("w2", 0, 0, "fwd")
+        group("w2", 0, 0, on_vector=False)
+        quantise("uh", 0)
+        flip("u2", 0, 0, "back")
+        group("u2", 0, 0, on_vector=True)
+        bias_ps = bank_tile("pre")
+        for e in range(2):
+            nc.tensor.transpose(bias_ps[:, e * P : (e + 1) * P], bias_rows_f[:, e::2], ident[:])
+        nc.scalar.copy(
+            out=bias_t[:].rearrange("p (e m) -> p e m", e=2),
+            in_=bias_ps[:, 0:SPAN].rearrange("p (e m) -> p e m", e=2)[:, :, 0 : 2 * SPANS],
+        )
+        quantise("w2", 0)
+        flip("w2", 1, 0, "back")
+        group("w2", 1, 0, on_vector=False)
         sz = const.tile([P, 1], F32, name="sz")
         sn = const.tile([P, 1], F32, name="sn")
         inv_sz = const.tile([P, 1], F32, name="inv_sz")
@@ -296,42 +345,6 @@ def tile_fastgrnncudacell_pa_t_kernel(
         one = const.tile([P, 1], F32, name="one")
         nc.scalar.activation(out=sz[:], in_=zeta_sb[:], func=ACT.Sigmoid)
         nc.scalar.activation(out=sn[:], in_=nu_sb[:], func=ACT.Sigmoid)
-        nc.vector.memset(one[:], 1.0)
-        nc.vector.tensor_add(out=sn[:], in0=sz[:], in1=sn[:])
-        nc.vector.tensor_scalar_max(out=sz[:], in0=sz[:], scalar1=SZ_FLOOR)
-        nc.vector.reciprocal(out=inv_sz[:], in_=sz[:])
-        nc.vector.tensor_scalar_mul(out=neg_sz[:], in0=sz[:], scalar1=-1.0)
-        nc.vector.tensor_mul(out=kappa[:], in0=sn[:], in1=inv_sz[:])
-        nc.vector.tensor_scalar_mul(out=neg_kappa[:], in0=kappa[:], scalar1=-1.0)
-
-        bias_rows_f = const.tile([P, SPAN], F32, name="bias_rows_f")
-        bias_t = const.tile([P, 4 * SPANS], F32, name="bias_t")
-        nc.vector.tensor_copy(out=bias_rows_f[:], in_=bias_rows[:])
-
-        flip("wx", 0, 0, "back")
-        group("wx", 0, 0, on_vector=False)
-        flip("wx", 0, 1, "back")
-        group("wx", 0, 1, on_vector=True)
-        bias_ps = bank_tile("pre")
-        for e in range(2):
-            nc.tensor.transpose(bias_ps[:, e * P : (e + 1) * P], bias_rows_f[:, e::2], ident[:])
-        nc.scalar.copy(
-            out=bias_t[:].rearrange("p (e m) -> p e m", e=2),
-            in_=bias_ps[:, 0:SPAN].rearrange("p (e m) -> p e m", e=2)[:, :, 0 : 2 * SPANS],
-        )
-        flip("uh", 0, 0, "st")
-        group("uh", 0, 0, on_vector=False)
-        quantise("wx", 0)
-        flip("uh", 0, 1, "st")
-        group("uh", 0, 1, on_vector=True)
-        flip("w2", 0, 0, "fwd")
-        group("w2", 0, 0, on_vector=False)
-        quantise("uh", 0)
-        flip("u2", 0, 0, "back")
-        group("u2", 0, 0, on_vector=True)
-        quantise("w2", 0)
-        flip("w2", 1, 0, "back")
-        group("w2", 1, 0, on_vector=False)
         quantise("u2", 0)
         flip("u2", 1, 0, "fwd")
         group("u2", 1, 0, on_vector=True)
@@ -339,6 +352,13 @@ def tile_fastgrnncudacell_pa_t_kernel(
         project(0, 1)
         quantise("w2", 1)
         quantise("u2", 1)
+        nc.vector.memset(one[:], 1.0)
+        nc.vector.tensor_add(out=sn[:], in0=sz[:], in1=sn[:])
+        nc.vector.tensor_scalar_max(out=sz[:], in0=sz[:], scalar1=SZ_FLOOR)
+        nc.vector.reciprocal(out=inv_sz[:], in_=sz[:])
+        nc.vector.tensor_scalar_mul(out=neg_sz[:], in0=sz[:], scalar1=-1.0)
+        nc.vector.tensor_mul(out=kappa[:], in0=sn[:], in1=inv_sz[:])
+        nc.vector.tensor_scalar_mul(out=neg_kappa[:], in0=kappa[:], scalar1=-1.0)
 
         def preparations(r):
             if r < 2:
@@ -353,7 +373,7 @@ def tile_fastgrnncudacell_pa_t_kernel(
         for r in range(STEPS + 3):
             c, j = divmod(r, SPANS)
             if j == 0 and c + 1 < CHUNKS:
-                load_state(c + 1)
+                load_state(c + 1, 0)
                 if c + 2 < CHUNKS:
                     load_operand("wx", c + 2)
                     load_operand("uh", c + 2)

@@ -199,7 +199,7 @@ def tile_fastgrnncudacell_pa_t_kernel(
             )
 
         def vector_only(r):
-            return r == 0
+            return r in (0, STEPS - 1)
 
         def product_vector(r):
             cols = slice(0, 2 * ROWS if vector_only(r) else V_COLS)
@@ -263,14 +263,19 @@ def tile_fastgrnncudacell_pa_t_kernel(
                 op0=ALU.mult, op1=ALU.add,
             )
 
-        def store(r):
+        def store(r, b):
             c, j = divmod(r, SPANS)
             spans = store_spans(c)
-            if (j + 1) % spans == 0:
-                nc.sync.dma_start(
-                    out=out_v[c][:, :, (j + 1 - spans) * SPAN : (j + 1) * SPAN],
-                    in_=out_sb[c, j // spans][:].rearrange("q (i d) -> q i d", i=BLOCKS),
-                )
+            if spans == 1:
+                blocks = slice(2 * b, 2 * b + 2)
+            elif b == 1 and (j + 1) % spans == 0:
+                blocks = slice(0, BLOCKS)
+            else:
+                return
+            nc.sync.dma_start(
+                out=out_v[c][:, blocks, (j + 1 - spans) * SPAN : (j + 1) * SPAN],
+                in_=out_sb[c, j // spans][:].rearrange("q (i d) -> q i d", i=BLOCKS)[:, blocks, :],
+            )
 
         zeros = const.tile([P, ROWS], BF16, name="zeros")
         nc.vector.memset(zeros[:], 0.0)
@@ -411,11 +416,11 @@ def tile_fastgrnncudacell_pa_t_kernel(
                 if on_vector:
                     group(kind, index, a, True)
             if r >= 3:
-                mix(r - 3, 0)
-                mix(r - 3, 1)
-                store(r - 3)
+                for b in range(2):
+                    mix(r - 3, b)
+                    store(r - 3, b)
+            if 1 <= r <= STEPS:
+                product_vector(r - 1)
             for kind, index, a, on_vector in prep:
                 if a == blocks_of[kind] // 2 - 1:
                     quantise(kind, index)
-            if 1 <= r <= STEPS:
-                product_vector(r - 1)

@@ -25,6 +25,7 @@ G_COLS = 528
 V_COLS = 2 * ROWS - G_COLS
 S_COLS = 208
 WARM_PASSES = 5
+SHIFTED = V_COLS - (G_COLS - S_COLS)
 SZ_FLOOR = 2.0 ** -13
 
 FLOPS = 2 * BATCH * HIDDEN * (2 * RANK)
@@ -210,21 +211,23 @@ def tile_fastgrnncudacell_pa_t_kernel(
 
         def shift_gpsimd(r):
             nc.gpsimd.tensor_scalar(
-                out=gate_t[r - 1][:, 0 : G_COLS - S_COLS], in0=gate_t[r][:, V_COLS : 2 * ROWS - S_COLS],
+                out=gate_t[r - 1][:, SHIFTED : SHIFTED + G_COLS - S_COLS],
+                in0=gate_t[r][:, V_COLS : 2 * ROWS - S_COLS],
                 scalar1=one[:, 0:1],
                 scalar2=neg_kappa[:, 0:1], op0=ALU.mult, op1=ALU.add,
             )
 
         def shift_scalar(r):
             nc.scalar.activation(
-                out=gate_t[r - 1][:, G_COLS - S_COLS : G_COLS], in_=gate_t[r][:, 2 * ROWS - S_COLS :],
+                out=gate_t[r - 1][:, SHIFTED + G_COLS - S_COLS : SHIFTED + G_COLS],
+                in_=gate_t[r][:, 2 * ROWS - S_COLS :],
                 func=ACT.Identity, bias=neg_kappa[:, 0:1], scale=1.0,
             )
 
         def product_gpsimd(r):
             nc.gpsimd.tensor_tensor(
-                out=cand_t[r][:, V_COLS:], in0=gate_t[r - 1][:, 0:G_COLS], in1=cand_t[r][:, V_COLS:],
-                op=ALU.mult,
+                out=cand_t[r][:, V_COLS:], in0=gate_t[r - 1][:, SHIFTED : SHIFTED + G_COLS],
+                in1=cand_t[r][:, V_COLS:], op=ALU.mult,
             )
 
         def flip_back(r):

@@ -133,16 +133,18 @@ def tile_fastgrnncudacell_pa_t_kernel(
             else:
                 nc.scalar.copy(out=dst, in_=src)
 
-        def quantise(kind, index):
-            rows = blocks_of[kind] * P
-            pool = moving_pool if kind in ("wx", "uh") else const
-            tag = kind if kind in ("wx", "uh") else "%s%d" % (kind, index)
-            codes[kind, index] = pool.tile([P, rows], U32, name="c_" + tag, tag="c_" + tag, align_bytes=64)
-            scales[kind, index] = pool.tile([P, rows], U8, name="s_" + tag, tag="s_" + tag, align_bytes=64)
+        def quantise(kind, index, first, last):
+            if first == 0:
+                rows = blocks_of[kind] * P
+                pool = moving_pool if kind in ("wx", "uh") else const
+                tag = kind if kind in ("wx", "uh") else "%s%d" % (kind, index)
+                codes[kind, index] = pool.tile([P, rows], U32, name="c_" + tag, tag="c_" + tag, align_bytes=64)
+                scales[kind, index] = pool.tile([P, rows], U8, name="s_" + tag, tag="s_" + tag, align_bytes=64)
+            part = slice(first * P, last * P)
             nc.vector.quantize_mx(
-                out=codes[kind, index][:].bitcast(FP8X4),
-                scales=scales[kind, index][:],
-                in_=grouped[kind, index][:, 0 : rows * PACK],
+                out=codes[kind, index][:, part].bitcast(FP8X4),
+                scales=scales[kind, index][:, part],
+                in_=grouped[kind, index][:, first * P * PACK : last * P * PACK],
             )
 
         pre = {}
@@ -323,7 +325,7 @@ def tile_fastgrnncudacell_pa_t_kernel(
         group("wx", 0, 1, on_vector=True)
         flip("uh", 0, 0, "st")
         group("uh", 0, 0, on_vector=False)
-        quantise("wx", 0)
+        quantise("wx", 0, 0, BLOCKS)
         flip("uh", 0, 1, "st")
         group("uh", 0, 1, on_vector=True)
         bias_rows_f = const.tile([P, SPAN], F32, name="bias_rows_f")
@@ -331,7 +333,7 @@ def tile_fastgrnncudacell_pa_t_kernel(
         nc.vector.tensor_copy(out=bias_rows_f[:], in_=bias_rows[:])
         flip("w2", 0, 0, "fwd")
         group("w2", 0, 0, on_vector=False)
-        quantise("uh", 0)
+        quantise("uh", 0, 0, BLOCKS)
         flip("u2", 0, 0, "back")
         group("u2", 0, 0, on_vector=True)
         bias_ps = bank_tile("pre")
@@ -341,7 +343,7 @@ def tile_fastgrnncudacell_pa_t_kernel(
             out=bias_t[:].rearrange("p (e m) -> p e m", e=2),
             in_=bias_ps[:, 0:SPAN].rearrange("p (e m) -> p e m", e=2)[:, :, 0 : 2 * SPANS],
         )
-        quantise("w2", 0)
+        quantise("w2", 0, 0, 2)
         flip("w2", 1, 0, "back")
         group("w2", 1, 0, on_vector=False)
         sz = const.tile([P, 1], F32, name="sz")
@@ -353,13 +355,13 @@ def tile_fastgrnncudacell_pa_t_kernel(
         one = const.tile([P, 1], F32, name="one")
         nc.scalar.activation(out=sz[:], in_=zeta_sb[:], func=ACT.Sigmoid)
         nc.scalar.activation(out=sn[:], in_=nu_sb[:], func=ACT.Sigmoid)
-        quantise("u2", 0)
+        quantise("u2", 0, 0, 2)
         flip("u2", 1, 0, "fwd")
         group("u2", 1, 0, on_vector=True)
         project(0, 0)
         project(0, 1)
-        quantise("w2", 1)
-        quantise("u2", 1)
+        quantise("w2", 1, 0, 2)
+        quantise("u2", 1, 0, 2)
         nc.vector.memset(one[:], 1.0)
         nc.vector.tensor_add(out=sn[:], in0=sz[:], in1=sn[:])
         nc.vector.tensor_scalar_max(out=sz[:], in0=sz[:], scalar1=SZ_FLOOR)
@@ -425,5 +427,4 @@ def tile_fastgrnncudacell_pa_t_kernel(
             if 1 <= r <= STEPS:
                 product_vector(r - 1)
             for kind, index, a, on_vector in prep:
-                if a == blocks_of[kind] // 2 - 1:
-                    quantise(kind, index)
+                quantise(kind, index, 2 * a, 2 * a + 2)

@@ -21,9 +21,9 @@ SPAN = 2 * P
 SPANS = HIDDEN // SPAN
 STEPS = CHUNKS * SPANS
 WORDS = RANK // 2
-G_COLS = 528
+G_COLS = 560
 V_COLS = 2 * ROWS - G_COLS
-S_COLS = 208
+S_COLS = 192
 WARM_PASSES = 5
 SHIFTED = V_COLS - (G_COLS - S_COLS)
 SZ_FLOOR = 2.0 ** -13
@@ -75,7 +75,11 @@ def tile_fastgrnncudacell_pa_t_kernel(
             else:
                 tile = raw_w_pool.tile([P, 2 * RANK], BF16, name="raw_w", tag="raw_w")
             raw[kind, index] = tile
-            nc.sync.dma_start(out=tile[:], in_=sources[kind][index])
+            pieces = 2 if kind in ("wx", "uh") and index == 0 else 1
+            width = blocks_of[kind] * RANK // pieces
+            for k in range(pieces):
+                cols = slice(k * width, (k + 1) * width)
+                nc.sync.dma_start(out=tile[:, cols], in_=sources[kind][index][:, cols])
 
         def state_spans(c):
             return 2 if c == 0 else SPANS

from contextlib import ExitStack

import concourse.mybir as mybir
from concourse.masks import make_identity

F32 = mybir.dt.float32
BF16 = mybir.dt.bfloat16
U32 = mybir.dt.uint32
U8 = mybir.dt.uint8
FP8X4 = mybir.dt.float8_e4m3fn_x4
ACT = mybir.ActivationFunctionType
ALU = mybir.AluOpType

P = 128
PACK = 4
BATCH, RANK, HIDDEN = 4096, 512, 1024
ROWS = 512
BLOCKS = ROWS // P
CHUNKS = BATCH // ROWS
SPAN = 2 * P
SPANS = HIDDEN // SPAN
STEPS = CHUNKS * SPANS
WORDS = RANK // 2
G_COLS = 560
V_COLS = 2 * ROWS - G_COLS
S_COLS = 192
WARM_PASSES = 5
SHIFTED = V_COLS - (G_COLS - S_COLS)
SZ_FLOOR = 2.0 ** -13

FLOPS = 2 * BATCH * HIDDEN * (2 * RANK)


def tile_fastgrnncudacell_pa_t_kernel(
    tc, wx_r, uh_r, state, W2, U2, bias_gate, bias_update, zeta, nu, out
):
    nc = tc.nc
    with ExitStack() as ctx:
        const = ctx.enter_context(tc.tile_pool(name="const", bufs=1))
        raw_w_pool = ctx.enter_context(tc.tile_pool(name="raw_w", bufs=8))
        raw_x_pool = ctx.enter_context(tc.tile_pool(name="raw_x", bufs=6))
        grouped_pool = ctx.enter_context(tc.tile_pool(name="grouped", bufs=3))
        moving_pool = ctx.enter_context(tc.tile_pool(name="moving", bufs=3))
        state_pool = ctx.enter_context(tc.tile_pool(name="state", bufs=3))
        gates_pool = ctx.enter_context(tc.tile_pool(name="gates", bufs=5))
        out_pool = ctx.enter_context(tc.tile_pool(name="outp", bufs=4))
        psum_pre = ctx.enter_context(tc.psum_pool(name="psum_pre", bufs=3))
        psum_fwd = ctx.enter_context(tc.psum_pool(name="psum_fwd", bufs=1))
        psum_state = ctx.enter_context(tc.psum_pool(name="psum_state", bufs=2))
        psum_back = ctx.enter_context(tc.psum_pool(name="psum_back", bufs=2))
        ctx.enter_context(tc.manual_schedule())

        batch_view = "(c p i) d -> c p (i d)"
        state_v = state.rearrange("(c p i) d -> c p i d", p=P, i=BLOCKS)
        out_v = out.rearrange("(c p i) d -> c p i d", p=P, i=BLOCKS)
        weight_view = "(j p e) k -> j p (e k)"
        sources = {
            "wx": wx_r.rearrange(batch_view, p=P, i=BLOCKS),
            "uh": uh_r.rearrange(batch_view, p=P, i=BLOCKS),
            "w2": W2.rearrange(weight_view, p=P, e=2),
            "u2": U2.rearrange(weight_view, p=P, e=2),
        }
        blocks_of = {"wx": BLOCKS, "uh": BLOCKS, "w2": 2, "u2": 2}

        raw = {}
        grouped = {}
        codes = {}
        scales = {}
        state_sb = {}
        out_sb = {}

        def load_operand(kind, index):
            if kind in ("wx", "uh"):
                tile = raw_x_pool.tile([P, BLOCKS * RANK], BF16, name="raw_x", tag="raw_x")
            else:
                tile = raw_w_pool.tile([P, 2 * RANK], BF16, name="raw_w", tag="raw_w")
            raw[kind, index] = tile
            pieces = 2 if kind in ("wx", "uh") and index == 0 else 1
            width = blocks_of[kind] * RANK // pieces
            for k in range(pieces):
                cols = slice(k * width, (k + 1) * width)
                nc.sync.dma_start(out=tile[:, cols], in_=sources[kind][index][:, cols])

        def state_spans(c):
            return 2 if c == 0 else SPANS

        def load_state(c, part):
            width = state_spans(c) * SPAN
            state_sb[c, part] = state_pool.tile(
                [P, BLOCKS * width], BF16, name="state_sb", tag="state_sb%d" % state_spans(c)
            )
            nc.sync.dma_start(
                out=state_sb[c, part][:].rearrange("q (i d) -> q i d", i=BLOCKS),
                in_=state_v[c][:, :, part * width : (part + 1) * width],
            )

        def state_span(r):
            c, j = divmod(r, SPANS)
            part, k = divmod(j, state_spans(c))
            tile = state_sb[c, part][:].rearrange("q (i d) -> q i d", i=BLOCKS)
            return tile[:, :, k * SPAN : (k + 1) * SPAN]

        def bank_tile(tag):
            if tag == "fwd":
                return psum_fwd.tile([P, ROWS], F32, name="fwd", tag="fwd")
            if tag == "st":
                return psum_state.tile([P, ROWS], F32, name="st", tag="st")
            if tag == "back":
                return psum_back.tile([P, ROWS], F32, name="back", tag="back")
            return psum_pre.tile([P, ROWS], F32, name="pre", tag="pre")

        flipped = {}

        def flip(kind, index, a, tag):
            words = raw[kind, index][:].bitcast(F32)
            bank = bank_tile(tag)
            for v in range(2):
                for b in range(2):
                    block = 2 * a + b
                    nc.tensor.transpose(
                        bank[:, (2 * v + b) * P : (2 * v + b + 1) * P],
                        words[:, block * WORDS + v : (block + 1) * WORDS : 2],
                        ident[:],
                    )
            flipped[kind, index, a] = bank

        def group(kind, index, a, on_vector):
            if a == 0:
                grouped[kind, index] = grouped_pool.tile(
                    [P, ROWS * PACK], BF16, name="grouped", tag="grouped", align_bytes=64
                )
            dst = grouped[kind, index][:].bitcast(F32).rearrange("p (n v) -> p n v", v=2)
            dst = dst[:, 2 * a * P : 2 * (a + 1) * P, :]
            src = flipped[kind, index, a][:].rearrange("p (v n) -> p n v", v=2)
            if on_vector:
                nc.vector.tensor_copy(out=dst, in_=src)
            else:
                nc.scalar.copy(out=dst, in_=src)

        def quantise(kind, index, first, last):
            if first == 0:
                rows = blocks_of[kind] * P
                pool = moving_pool if kind in ("wx", "uh") else const
                tag = kind if kind in ("wx", "uh") else "%s%d" % (kind, index)
                codes[kind, index] = pool.tile([P, rows], U32, name="c_" + tag, tag="c_" + tag, align_bytes=64)
                scales[kind, index] = pool.tile([P, rows], U8, name="s_" + tag, tag="s_" + tag, align_bytes=64)
            part = slice(first * P, last * P)
            nc.vector.quantize_mx(
                out=codes[kind, index][:, part].bitcast(FP8X4),
                scales=scales[kind, index][:, part],
                in_=grouped[kind, index][:, first * P * PACK : last * P * PACK],
            )

        pre = {}
        gate_t = {}
        cand_t = {}
        state_ps = {}
        back = {}

        def project(r, e):
            c, j = divmod(r, SPANS)
            pre[r, e] = bank_tile("pre")
            pairs = ((("w2", j), ("wx", c)), (("u2", j), ("uh", c)))
            for n, (weight, moving) in enumerate(pairs):
                nc.tensor.matmul_mx(
                    out=pre[r, e][:],
                    lhsT=codes[weight][:, e * P : (e + 1) * P].bitcast(FP8X4),
                    lhsT_scale=scales[weight][:, e * P : (e + 1) * P],
                    rhs=codes[moving][:].bitcast(FP8X4),
                    rhs_scale=scales[moving][:],
                    start=(n == 0),
                    stop=(n == 1),
                )

        def activate(r, e, which):
            j = r % SPANS
            cols = slice(e * ROWS, (e + 1) * ROWS)
            if which == "tanh":
                column = 2 * SPANS * e + SPANS + j
                nc.scalar.activation(
                    out=cand_t[r][:, cols], in_=pre[r, e][:], func=ACT.Tanh,
                    bias=bias_t[:, column : column + 1], scale=1.0,
                )
            else:
                column = 2 * SPANS * e + j
                nc.scalar.activation(
                    out=gate_t[r][:, cols], in_=pre[r, e][:], func=ACT.Sigmoid,
                    bias=bias_t[:, column : column + 1], scale=1.0,
                )

        def flip_state(r):
            state_ps[r] = bank_tile("st")
            for i in range(BLOCKS):
                nc.tensor.transpose(
                    state_ps[r][:, i * P : (i + 1) * P], state_span(r)[:, i, :].bitcast(F32), ident[:]
                )

        def subtract(r):
            view = "p (e n) -> p e n"
            nc.vector.scalar_tensor_tensor(
                out=cand_t[r][:].rearrange(view, e=2),
                in0=cand_t[r][:].rearrange(view, e=2),
                scalar=neg_sz[:, 0:1],
                in1=state_ps[r][:].bitcast(BF16).rearrange("p (n e) -> p e n", e=2),
                op0=ALU.mult, op1=ALU.add,
            )

        def vector_only(r):
            return r in (0, STEPS - 1)

        def product_vector(r):
            cols = slice(0, 2 * ROWS if vector_only(r) else V_COLS)
            nc.vector.scalar_tensor_tensor(
                out=cand_t[r][:, cols], in0=gate_t[r][:, cols], scalar=kappa[:, 0:1],
                in1=cand_t[r][:, cols], op0=ALU.subtract, op1=ALU.mult,
            )

        def shift_gpsimd(r):
            nc.gpsimd.tensor_scalar(
                out=gate_t[r - 1][:, SHIFTED : SHIFTED + G_COLS - S_COLS],
                in0=gate_t[r][:, V_COLS : 2 * ROWS - S_COLS],
                scalar1=one[:, 0:1],
                scalar2=neg_kappa[:, 0:1], op0=ALU.mult, op1=ALU.add,
            )

        def shift_scalar(r):
            nc.scalar.activation(
                out=gate_t[r - 1][:, SHIFTED + G_COLS - S_COLS : SHIFTED + G_COLS],
                in_=gate_t[r][:, 2 * ROWS - S_COLS :],
                func=ACT.Identity, bias=neg_kappa[:, 0:1], scale=1.0,
            )

        def product_gpsimd(r):
            nc.gpsimd.tensor_tensor(
                out=cand_t[r][:, V_COLS:], in0=gate_t[r - 1][:, SHIFTED : SHIFTED + G_COLS],
                in1=cand_t[r][:, V_COLS:], op=ALU.mult,
            )

        def flip_back(r):
            for b in range(2):
                back[r, b] = bank_tile("back")
                for i in range(2):
                    for e in range(2):
                        first = e * ROWS + (2 * b + i) * P
                        nc.tensor.transpose(
                            back[r, b][:, (2 * e + i) * P : (2 * e + i + 1) * P],
                            cand_t[r][:, first : first + P],
                            ident[:],
                        )

        def store_spans(c):
            return 2 if c < CHUNKS - 1 else 1

        def mix(r, b):
            c, j = divmod(r, SPANS)
            group_first, half = divmod(j, store_spans(c))
            if half == 0 and b == 0:
                out_sb[c, group_first] = out_pool.tile(
                    [P, BLOCKS * store_spans(c) * SPAN], F32, name="out_sb", tag="out_sb"
                )
            block_view = "q (i d) -> q i d"
            pair_view = "q i (p e) -> q i p e"
            blocks = slice(2 * b, 2 * b + 2)
            state_part = state_span(r)[:, blocks, :]
            out_part = out_sb[c, group_first][:].rearrange(block_view, i=BLOCKS)
            out_part = out_part[:, blocks, half * SPAN : (half + 1) * SPAN]
            nc.vector.scalar_tensor_tensor(
                out=out_part.rearrange(pair_view, e=2),
                in0=state_part.rearrange(pair_view, e=2),
                scalar=kappa[:, 0:1],
                in1=back[r, b][:].rearrange("q (e i p) -> q i p e", i=2, e=2),
                op0=ALU.mult, op1=ALU.add,
            )

        def store(r, b):
            c, j = divmod(r, SPANS)
            spans = store_spans(c)
            if spans == 1:
                blocks = slice(2 * b, 2 * b + 2)
            elif b == 1 and (j + 1) % spans == 0:
                blocks = slice(0, BLOCKS)
            else:
                return
            nc.sync.dma_start(
                out=out_v[c][:, blocks, (j + 1 - spans) * SPAN : (j + 1) * SPAN],
                in_=out_sb[c, j // spans][:].rearrange("q (i d) -> q i d", i=BLOCKS)[:, blocks, :],
            )

        zeros = const.tile([P, ROWS], BF16, name="zeros")
        nc.vector.memset(zeros[:], 0.0)

        load_operand("wx", 0)
        load_operand("uh", 0)
        load_operand("w2", 0)
        load_operand("u2", 0)
        zeta_sb = const.tile([P, 1], BF16, name="zeta_sb")
        nu_sb = const.tile([P, 1], BF16, name="nu_sb")
        bias_rows = const.tile([P, SPAN], BF16, name="bias_rows")
        nc.gpsimd.memset(bias_rows[:], 0.0)
        row_view = "o (j m) -> (o j) m"
        nc.scalar.dma_start(out=bias_rows[0:SPANS, :], in_=bias_gate.rearrange(row_view, m=SPAN))
        nc.scalar.dma_start(
            out=bias_rows[SPANS : 2 * SPANS, :], in_=bias_update.rearrange(row_view, m=SPAN)
        )
        nc.scalar.dma_start(out=zeta_sb[:], in_=zeta.to_broadcast([P, 1]))
        nc.scalar.dma_start(out=nu_sb[:], in_=nu.to_broadcast([P, 1]))
        ident = const.tile([P, P], F32, name="ident")
        make_identity(nc, ident[:])
        load_operand("w2", 1)
        load_operand("u2", 1)
        load_state(0, 0)
        load_operand("w2", 2)
        load_operand("u2", 2)
        load_operand("wx", 1)
        load_operand("w2", 3)
        load_operand("u2", 3)
        load_state(0, 1)
        load_operand("uh", 1)

        unused = const.tile([P, 1], F32, name="unused")
        nc.scalar.activation(out=unused[:], in_=zeros[:, 0:1], func=ACT.Sigmoid)
        warm_ps = bank_tile("pre")
        for k in range(WARM_PASSES):
            nc.tensor.matmul(out=warm_ps[:], lhsT=zeros[:, 0:P], rhs=zeros[:], start=True, stop=True)

        flip("wx", 0, 0, "back")
        group("wx", 0, 0, on_vector=False)
        flip("wx", 0, 1, "back")
        group("wx", 0, 1, on_vector=True)
        flip("uh", 0, 0, "st")
        group("uh", 0, 0, on_vector=False)
        quantise("wx", 0, 0, BLOCKS)
        flip("uh", 0, 1, "st")
        group("uh", 0, 1, on_vector=True)
        bias_rows_f = const.tile([P, SPAN], F32, name="bias_rows_f")
        bias_t = const.tile([P, 4 * SPANS], F32, name="bias_t")
        nc.vector.tensor_copy(out=bias_rows_f[:], in_=bias_rows[:])
        flip("w2", 0, 0, "fwd")
        group("w2", 0, 0, on_vector=False)
        quantise("uh", 0, 0, BLOCKS)
        flip("u2", 0, 0, "back")
        group("u2", 0, 0, on_vector=True)
        bias_ps = bank_tile("pre")
        for e in range(2):
            nc.tensor.transpose(bias_ps[:, e * P : (e + 1) * P], bias_rows_f[:, e::2], ident[:])
        nc.scalar.copy(
            out=bias_t[:].rearrange("p (e m) -> p e m", e=2),
            in_=bias_ps[:, 0:SPAN].rearrange("p (e m) -> p e m", e=2)[:, :, 0 : 2 * SPANS],
        )
        quantise("w2", 0, 0, 2)
        flip("w2", 1, 0, "back")
        group("w2", 1, 0, on_vector=False)
        sz = const.tile([P, 1], F32, name="sz")
        sn = const.tile([P, 1], F32, name="sn")
        inv_sz = const.tile([P, 1], F32, name="inv_sz")
        kappa = const.tile([P, 1], F32, name="kappa")
        neg_sz = const.tile([P, 1], F32, name="neg_sz")
        neg_kappa = const.tile([P, 1], F32, name="neg_kappa")
        one = const.tile([P, 1], F32, name="one")
        nc.scalar.activation(out=sz[:], in_=zeta_sb[:], func=ACT.Sigmoid)
        nc.scalar.activation(out=sn[:], in_=nu_sb[:], func=ACT.Sigmoid)
        quantise("u2", 0, 0, 2)
        flip("u2", 1, 0, "fwd")
        group("u2", 1, 0, on_vector=True)
        project(0, 0)
        project(0, 1)
        quantise("w2", 1, 0, 2)
        quantise("u2", 1, 0, 2)
        nc.vector.memset(one[:], 1.0)
        nc.vector.tensor_add(out=sn[:], in0=sz[:], in1=sn[:])
        nc.vector.tensor_scalar_max(out=sz[:], in0=sz[:], scalar1=SZ_FLOOR)
        nc.vector.reciprocal(out=inv_sz[:], in_=sz[:])
        nc.vector.tensor_scalar_mul(out=neg_sz[:], in0=sz[:], scalar1=-1.0)
        nc.vector.tensor_mul(out=kappa[:], in0=sn[:], in1=inv_sz[:])
        nc.vector.tensor_scalar_mul(out=neg_kappa[:], in0=kappa[:], scalar1=-1.0)

        def preparations(r):
            if r < 2:
                return [("w2", r + 2, 0, True), ("u2", r + 2, 0, False), ("wx", 1, r, r == 0)]
            if r == 2:
                return [("uh", 1, 0, False), ("uh", 1, 1, True)]
            c, k = divmod(r - 3, SPANS)
            if c + 2 < CHUNKS:
                return [("wx" if k < 2 else "uh", c + 2, k % 2, False)]
            return []

        for r in range(STEPS + 3):
            c, j = divmod(r, SPANS)
            if j == 0 and c + 1 < CHUNKS:
                load_state(c + 1, 0)
                if c + 2 < CHUNKS:
                    load_operand("wx", c + 2)
                    load_operand("uh", c + 2)
            prep = preparations(r)
            for n, (kind, index, a, on_vector) in enumerate(prep):
                flip(kind, index, a, "back" if n > 0 else "fwd")
            if r < STEPS:
                flip_state(r)
            if r >= 3:
                flip_back(r - 3)
            if r + 1 < STEPS:
                project(r + 1, 0)
            if r < STEPS:
                gate_t[r] = gates_pool.tile([P, 2 * ROWS], F32, name="gate_t", tag="gate_t")
                cand_t[r] = gates_pool.tile([P, 2 * ROWS], F32, name="cand_t", tag="cand_t")
                activate(r, 0, "tanh")
                activate(r, 0, "sigmoid")
                activate(r, 1, "tanh")
            if 1 <= r <= STEPS and not vector_only(r - 1):
                shift_scalar(r - 1)
            for kind, index, a, on_vector in prep:
                if not on_vector:
                    group(kind, index, a, False)
            if r < STEPS:
                activate(r, 1, "sigmoid")
            if r + 1 < STEPS:
                project(r + 1, 1)
            if 1 <= r <= STEPS:
                subtract(r - 1)
                if not vector_only(r - 1):
                    shift_gpsimd(r - 1)
            if 2 <= r <= STEPS + 1 and not vector_only(r - 2):
                product_gpsimd(r - 2)
            for kind, index, a, on_vector in prep:
                if on_vector:
                    group(kind, index, a, True)
            if r >= 3:
                for b in range(2):
                    mix(r - 3, b)
                    store(r - 3, b)
            if 1 <= r <= STEPS:
                product_vector(r - 1)
            for kind, index, a, on_vector in prep:
                quantise(kind, index, 2 * a, 2 * a + 2)
